import numpy as np
import ml_dtypes


def mxq(x, axis, fmt="e4m3"):
    dtype, down = {"e4m3": (ml_dtypes.float8_e4m3fn, 7), "e5m2": (ml_dtypes.float8_e5m2, 14)}[fmt]
    v = np.moveaxis(np.asarray(x, np.float32).astype(ml_dtypes.bfloat16).astype(np.float64), axis, -1)
    blocks = v.reshape(v.shape[:-1] + (-1, 32))
    amax = np.abs(blocks).max(-1, keepdims=True)
    byte = np.maximum(np.where(amax > 0, np.frexp(amax)[1] - 1 + 127, 0) - down, 1)
    scale = np.exp2(byte - 127.0)
    codes = (blocks / scale).astype(np.float32).astype(dtype).astype(np.float64)
    return np.moveaxis((codes * scale).reshape(v.shape), -1, axis)


WIDE = False


def mx_kscale(k):
    if not WIDE:
        return np.ones(k)
    levels = np.array([10, -10, 5, -5, 0])
    a = np.random.permutation(np.resize(levels, k // 512 * 4)).reshape(k // 512, 4)
    idx = np.arange(k)
    return np.exp2(a[idx // 512, idx % 128 // 32])


BF16 = ml_dtypes.bfloat16


def bf(x):
    return np.asarray(x, np.float32).astype(BF16)


def f64(x):
    return np.asarray(x).astype(np.float64)


B, S, D = 2, 1024, 1024
EPS = 1e-8


def layer_norm(v, w, b):
    mu = v.mean(-1, keepdims=True)
    var = ((v - mu) ** 2).mean(-1, keepdims=True)
    return (v - mu) / np.sqrt(var + EPS) * w + b


def setup_inputs():
    s = mx_kscale(D)
    xr = np.random.standard_normal((B, S, D)) + np.random.uniform(-1.2, 1.2, (B, S, 1))
    xi = np.random.standard_normal((B, S, D)) + np.random.uniform(-1.2, 1.2, (B, S, 1))
    return {"x_real": bf(xr * s), "x_imag": bf(xi * s),
            "phase_matrix": bf(np.random.standard_normal((D, D)) / np.sqrt(D) / s[:, None]),
            "coherence_factor": bf(np.random.uniform(0.35, 0.5, 1)),
            "ln_weight": bf(1.0 + 0.1 * np.random.standard_normal(D)),
            "ln_bias": bf(0.3 * np.random.standard_normal(D))}


def reference(x_real, x_imag, phase_matrix, coherence_factor, ln_weight, ln_bias):
    xr, xi = f64(x_real), f64(x_imag)
    a, b = xr + EPS, xi + EPS
    r = np.sqrt(a * a + b * b)
    sc = (a / r).sum(-1, keepdims=True)
    ss = (b / r).sum(-1, keepdims=True)
    coherence = (sc * sc + ss * ss) / (D * D)
    p = mxq(xr, 2, "e4m3") @ mxq(f64(phase_matrix), 0, "e4m3")
    p = p * f64(coherence_factor) * (1.0 - coherence)
    c, sn = np.cos(p), np.sin(p)
    new_real = xr * c - xi * sn
    new_imag = xr * sn + xi * c
    norm = np.sqrt(new_real ** 2 + new_imag ** 2 + EPS)
    new_real = new_real / norm
    new_imag = new_imag / norm
    w, bb = f64(ln_weight), f64(ln_bias)
    return (layer_norm(new_real, w, bb), layer_norm(new_imag, w, bb))

@@ -1,0 +1,244 @@
+import math
+from contextlib import ExitStack
+
+import concourse.mybir as mybir
+from concourse.masks import make_identity
+
+F32 = mybir.dt.float32
+BF16 = mybir.dt.bfloat16
+I32 = mybir.dt.int32
+U32 = mybir.dt.uint32
+U8 = mybir.dt.uint8
+FP8X4 = mybir.dt.float8_e4m3fn_x4
+ACT = mybir.ActivationFunctionType
+ALU = mybir.AluOpType
+
+P = 128
+D = 1024
+ROWS = 2048
+NT = ROWS // P
+HALF = 512
+EPS = 1e-8
+FLOPS = 2 * ROWS * D * D
+
+
+def tile_quantumcoherencelayer_kernel(
+    tc, x_real, x_imag, phase_matrix, coherence_factor, ln_weight, ln_bias, out_0, out_1
+):
+    nc = tc.nc
+    xr_d = x_real.flatten_outer_dims().rearrange("(t p) d -> t p d", p=P)
+    xi_d = x_imag.flatten_outer_dims().rearrange("(t p) d -> t p d", p=P)
+    o0_d = out_0.flatten_outer_dims().rearrange("(t p) d -> t p d", p=P)
+    o1_d = out_1.flatten_outer_dims().rearrange("(t p) d -> t p d", p=P)
+
+    with ExitStack() as ctx:
+        keep = ctx.enter_context(tc.tile_pool(name="keep", bufs=1))
+        cpsum = ctx.enter_context(tc.psum_pool(name="cpsum", bufs=1))
+
+        ident = keep.tile([P, P], F32)
+        make_identity(nc, ident[:])
+        eps_t = keep.tile([P, 1], F32)
+        nc.vector.memset(eps_t[:], EPS)
+        neghalf = keep.tile([P, 2], F32)
+        nc.vector.memset(neghalf[:], -0.5)
+
+        cfb = keep.tile([P, 1], BF16)
+        with nc.allow_non_contiguous_dma(reason="one bfloat16 scalar to every partition"):
+            nc.scalar.dma_start(out=cfb[:], in_=coherence_factor.partition_broadcast(P))
+        cf32 = keep.tile([P, 1], F32)
+        nc.vector.tensor_copy(out=cf32[:], in_=cfb[:])
+
+        pcodes = keep.tile([P, 2, D], U32, align_bytes=64)
+        pscales = keep.tile([P, 2, D], U8, align_bytes=64)
+        xcodes = keep.tile([P, NT, 2 * P], U32, align_bytes=64)
+        xscales = keep.tile([P, NT, 2 * P], U8, align_bytes=64)
+        sc = keep.tile([P, NT], F32)
+        ss = keep.tile([P, NT], F32)
+        gp = keep.tile([P, NT], F32)
+        cr_all = [keep.tile([P, D], F32, name="cr%d" % i) for i in range(NT)]
+        nci_all = [keep.tile([P, D], F32, name="nci%d" % i) for i in range(NT)]
+
+        wps = cpsum.tile([P, D], BF16)
+        bps = cpsum.tile([P, D], BF16)
+
+        with tc.tile_pool(name="stage", bufs=1) as stage, tc.tile_pool(name="xin", bufs=3) as xin, tc.tile_pool(
+            name="worka", bufs=2
+        ) as worka, tc.psum_pool(name="tpsum", bufs=2) as tpsum:
+            rows = stage.tile([P, 2 * D], BF16)
+            nc.vector.memset(rows[:], 0.0)
+            nc.scalar.dma_start(out=rows[0:1, 0:D], in_=ln_weight.rearrange("(o d) -> o d", o=1))
+            nc.scalar.dma_start(out=rows[0:1, D : 2 * D], in_=ln_bias.rearrange("(o d) -> o d", o=1))
+            ones = stage.tile([P, P], BF16)
+            nc.vector.memset(ones[:], 1.0)
+            for h in range(2):
+                nc.tensor.matmul(
+                    out=wps[:, h * HALF : (h + 1) * HALF],
+                    lhsT=ones[:],
+                    rhs=rows[:, h * HALF : (h + 1) * HALF],
+                    start=True,
+                    stop=True,
+                )
+            for h in range(2):
+                nc.tensor.matmul(
+                    out=bps[:, h * HALF : (h + 1) * HALF],
+                    lhsT=ones[:],
+                    rhs=rows[:, D + h * HALF : D + (h + 1) * HALF],
+                    start=True,
+                    stop=True,
+                )
+
+            for i in range(NT):
+                xr = xin.tile([P, D], BF16, tag="xr")
+                nc.sync.dma_start(out=xr[:], in_=xr_d[i])
+                xi = xin.tile([P, D], BF16, tag="xi")
+                nc.sync.dma_start(out=xi[:], in_=xi_d[i])
+
+                if i == 1:
+                    for g in range(2):
+                        raw = stage.tile([P, 4, D], BF16, tag="raw")
+                        for u in range(2):
+                            k0 = 512 * g + 256 * u
+                            nc.sync.dma_start(
+                                out=raw[:, 2 * u : 2 * u + 2, :],
+                                in_=phase_matrix[k0 : k0 + 256, :].rearrange("(q e) c -> q e c", e=2),
+                            )
+                        pg = stage.tile([P, D, 4], BF16, tag="pg", align_bytes=64)
+                        nc.vector.tensor_copy(
+                            out=pg[:].rearrange("p (c i) t -> p c t i", i=4),
+                            in_=raw[:].rearrange("p t (c i) -> p c t i", i=4),
+                        )
+                        nc.vector.quantize_mx(
+                            out=pcodes[:, g, :].bitcast(FP8X4),
+                            scales=pscales[:, g, :],
+                            in_=pg[:].rearrange("p c t -> p (c t)"),
+                        )
+
+                xt = tpsum.tile([P, 4 * P], F32, tag="xt")
+                xw = xr[:].bitcast(F32)
+                for j in range(4):
+                    nc.tensor.transpose(out=xt[:, j * P : (j + 1) * P], in_=xw[:, j * P : (j + 1) * P], identity=ident[:])
+                grouped = worka.tile([P, 2, P, 4], BF16, tag="grouped", align_bytes=64)
+                nc.scalar.copy(
+                    out=grouped[:].bitcast(F32),
+                    in_=xt[:].rearrange("p (g u r) -> p g r u", g=2, u=2),
+                )
+
+                sa = worka.tile([P, D], F32, tag="sa")
+                sb = worka.tile([P, D], F32, tag="sb")
+                sr = worka.tile([P, D], F32, tag="sr")
+                si = worka.tile([P, D], F32, tag="si")
+                nc.scalar.activation(out=sa[:], in_=xr[:], func=ACT.Square, bias=eps_t[:, 0:1], scale=1.0)
+                nc.scalar.activation(out=sb[:], in_=xi[:], func=ACT.Square, bias=eps_t[:, 0:1], scale=1.0)
+                nc.scalar.activation(out=sr[:], in_=xr[:], func=ACT.Square)
+                nc.scalar.activation(out=si[:], in_=xi[:], func=ACT.Square)
+                nc.vector.tensor_tensor(out=sa[:], in0=sa[:], in1=sb[:], op=ALU.add)
+                nc.vector.tensor_tensor(out=sr[:], in0=sr[:], in1=si[:], op=ALU.add)
+                nc.vector.quantize_mx(
+                    out=xcodes[:, i, :].bitcast(FP8X4),
+                    scales=xscales[:, i, :],
+                    in_=grouped[:].rearrange("p g r t -> p (g r t)"),
+                )
+                nc.scalar.activation(out=sa[:], in_=sa[:], func=ACT.Abs_reciprocal_sqrt)
+                nc.scalar.activation(out=sr[:], in_=sr[:], func=ACT.Abs_reciprocal_sqrt, bias=eps_t[:, 0:1], scale=1.0)
+                nc.vector.scalar_tensor_tensor(
+                    out=sb[:], in0=xr[:], scalar=EPS, in1=sa[:], op0=ALU.add, op1=ALU.mult, accum_out=sc[:, i : i + 1]
+                )
+                nc.vector.scalar_tensor_tensor(
+                    out=si[:], in0=xi[:], scalar=EPS, in1=sa[:], op0=ALU.add, op1=ALU.mult, accum_out=ss[:, i : i + 1]
+                )
+                nc.vector.tensor_tensor(out=cr_all[i][:], in0=xr[:], in1=sr[:], op=ALU.mult)
+                nc.vector.scalar_tensor_tensor(
+                    out=nci_all[i][:], in0=xi[:], scalar=-1.0, in1=sr[:], op0=ALU.mult, op1=ALU.mult
+                )
+
+            nc.vector.tensor_tensor(out=sc[:], in0=sc[:], in1=sc[:], op=ALU.mult)
+            nc.vector.tensor_tensor(out=ss[:], in0=ss[:], in1=ss[:], op=ALU.mult)
+            nc.vector.tensor_tensor(out=sc[:], in0=sc[:], in1=ss[:], op=ALU.add)
+            nc.vector.tensor_scalar(
+                out=sc[:], in0=sc[:], scalar1=-1.0 / (D * D), scalar2=1.0, op0=ALU.mult, op1=ALU.add
+            )
+            nc.vector.tensor_scalar(
+                out=gp[:], in0=sc[:], scalar1=cf32[:, 0:1], scalar2=1.0 / (2.0 * math.pi), op0=ALU.mult, op1=ALU.mult
+            )
+
+        with tc.tile_pool(name="workb", bufs=2) as workb, tc.tile_pool(name="stat", bufs=4) as stat, tc.psum_pool(
+            name="ppsum", bufs=2
+        ) as ppsum:
+            for i in range(NT):
+                g_i = gp[:, i : i + 1]
+                p0 = [ppsum.tile([P, HALF], F32, name="p0_%d" % n, tag="p0_%d" % n) for n in range(2)]
+                for n in range(2):
+                    for g in range(2):
+                        nc.tensor.matmul_mx(
+                            out=p0[n][:],
+                            lhsT=xcodes[:, i, g * P : (g + 1) * P].bitcast(FP8X4),
+                            lhsT_scale=xscales[:, i, g * P : (g + 1) * P],
+                            rhs=pcodes[:, g, n * HALF : (n + 1) * HALF].bitcast(FP8X4),
+                            rhs_scale=pscales[:, g, n * HALF : (n + 1) * HALF],
+                            start=(g == 0),
+                            stop=(g == 1),
+                        )
+                ki = workb.tile([P, D], I32, tag="ki")
+                v = workb.tile([P, D], F32, tag="v")
+                for n in range(2):
+                    cols = slice(n * HALF, (n + 1) * HALF)
+                    nc.vector.tensor_scalar(
+                        out=ki[:, cols], in0=p0[n][:], scalar1=g_i, scalar2=None, op0=ALU.mult
+                    )
+                for n in range(2):
+                    cols = slice(n * HALF, (n + 1) * HALF)
+                    nc.vector.scalar_tensor_tensor(
+                        out=v[:, cols], in0=p0[n][:], scalar=g_i, in1=ki[:, cols], op0=ALU.mult, op1=ALU.subtract
+                    )
+                s = workb.tile([P, D], F32, tag="s")
+                h = workb.tile([P, D], F32, tag="h")
+                nc.scalar.activation(out=h[:], in_=v[:], func=ACT.Sin, scale=math.pi)
+                nc.scalar.activation(out=s[:], in_=v[:], func=ACT.Sin, scale=2.0 * math.pi)
+                nc.scalar.activation(out=h[:], in_=h[:], func=ACT.Square, scale=math.sqrt(2.0))
+
+                fa = workb.tile([P, D], F32, tag="fa")
+                fb = workb.tile([P, D], F32, tag="fb")
+                sa2 = workb.tile([P, D], F32, tag="sa2")
+                sb2 = workb.tile([P, D], F32, tag="sb2")
+                nc.vector.scalar_tensor_tensor(
+                    out=fa[:], in0=h[:], scalar=1.0, in1=cr_all[i][:], op0=ALU.subtract, op1=ALU.mult
+                )
+                nc.vector.scalar_tensor_tensor(
+                    out=fb[:], in0=h[:], scalar=1.0, in1=nci_all[i][:], op0=ALU.subtract, op1=ALU.mult
+                )
+                nc.vector.tensor_tensor(out=sb2[:], in0=s[:], in1=nci_all[i][:], op=ALU.mult)
+                nc.vector.tensor_tensor(out=sa2[:], in0=s[:], in1=cr_all[i][:], op=ALU.mult)
+                sums = stat.tile([P, 2], F32, tag="sums")
+                nmu = stat.tile([P, 2], F32, tag="nmu")
+                sq = stat.tile([P, 2], F32, tag="sq")
+                var = stat.tile([P, 2], F32, tag="var")
+                rstd = stat.tile([P, 2], F32, tag="rstd")
+                nc.vector.scalar_tensor_tensor(
+                    out=sb2[:], in0=sb2[:], scalar=1.0, in1=fa[:], op0=ALU.mult, op1=ALU.subtract, accum_out=sums[:, 0:1]
+                )
+                nc.vector.scalar_tensor_tensor(
+                    out=sa2[:], in0=sa2[:], scalar=1.0, in1=fb[:], op0=ALU.mult, op1=ALU.add, accum_out=sums[:, 1:2]
+                )
+                nc.vector.tensor_scalar(out=nmu[:], in0=sums[:], scalar1=-1.0 / D, scalar2=None, op0=ALU.mult)
+                nc.scalar.activation(
+                    out=h[:], in_=sb2[:], func=ACT.Square, bias=nmu[:, 0:1], scale=1.0, accum_out=sq[:, 0:1]
+                )
+                nc.scalar.activation(
+                    out=h[:], in_=sa2[:], func=ACT.Square, bias=nmu[:, 1:2], scale=1.0, accum_out=sq[:, 1:2]
+                )
+                nc.gpsimd.tensor_scalar(out=var[:], in0=sq[:], scalar1=1.0 / D, scalar2=EPS, op0=ALU.mult, op1=ALU.add)
+                nc.gpsimd.tensor_tensor(out=rstd[:], in0=var[:], in1=neghalf[:], op=ALU.pow)
+                nc.vector.scalar_tensor_tensor(
+                    out=fa[:], in0=sb2[:], scalar=nmu[:, 0:1], in1=wps[:], op0=ALU.add, op1=ALU.mult
+                )
+                nc.vector.scalar_tensor_tensor(
+                    out=fa[:], in0=fa[:], scalar=rstd[:, 0:1], in1=bps[:], op0=ALU.mult, op1=ALU.add
+                )
+                nc.sync.dma_start(out=o0_d[i], in_=fa[:])
+                nc.vector.scalar_tensor_tensor(
+                    out=fb[:], in0=sa2[:], scalar=nmu[:, 1:2], in1=wps[:], op0=ALU.add, op1=ALU.mult
+                )
+                nc.vector.scalar_tensor_tensor(
+                    out=fb[:], in0=fb[:], scalar=rstd[:, 1:2], in1=bps[:], op0=ALU.mult, op1=ALU.add
+                )
+                nc.sync.dma_start(out=o1_d[i], in_=fb[:])

@@ -163,82 +163,122 @@ def tile_quantumcoherencelayer_kernel(
 
         with tc.tile_pool(name="workb", bufs=2) as workb, tc.tile_pool(name="stat", bufs=4) as stat, tc.psum_pool(
             name="ppsum", bufs=2
-        ) as ppsum:
-            for i in range(NT):
-                g_i = gp[:, i : i + 1]
-                p0 = [ppsum.tile([P, HALF], F32, name="p0_%d" % n, tag="p0_%d" % n) for n in range(2)]
-                for n in range(2):
-                    for g in range(2):
-                        nc.tensor.matmul_mx(
-                            out=p0[n][:],
-                            lhsT=xcodes[:, i, g * P : (g + 1) * P].bitcast(FP8X4),
-                            lhsT_scale=xscales[:, i, g * P : (g + 1) * P],
-                            rhs=pcodes[:, g, n * HALF : (n + 1) * HALF].bitcast(FP8X4),
-                            rhs_scale=pscales[:, g, n * HALF : (n + 1) * HALF],
-                            start=(g == 0),
-                            stop=(g == 1),
-                        )
-                ki = workb.tile([P, D], I32, tag="ki")
-                v = workb.tile([P, D], F32, tag="v")
-                for n in range(2):
-                    cols = slice(n * HALF, (n + 1) * HALF)
-                    nc.vector.tensor_scalar(
-                        out=ki[:, cols], in0=p0[n][:], scalar1=g_i, scalar2=None, op0=ALU.mult
-                    )
-                for n in range(2):
-                    cols = slice(n * HALF, (n + 1) * HALF)
-                    nc.vector.scalar_tensor_tensor(
-                        out=v[:, cols], in0=p0[n][:], scalar=g_i, in1=ki[:, cols], op0=ALU.mult, op1=ALU.subtract
-                    )
-                s = workb.tile([P, D], F32, tag="s")
-                h = workb.tile([P, D], F32, tag="h")
-                nc.scalar.activation(out=h[:], in_=v[:], func=ACT.Sin, scale=math.pi)
-                nc.scalar.activation(out=s[:], in_=v[:], func=ACT.Sin, scale=2.0 * math.pi)
-                nc.scalar.activation(out=h[:], in_=h[:], func=ACT.Square, scale=math.sqrt(2.0))
+        ) as ppsum, tc.manual_schedule():
+            p0 = {}
+            vs = {}
+            hh = {}
+            fa = {}
+            fb = {}
+            sa2 = {}
+            sb2 = {}
+            sums = {}
+            nmu = {}
+            sq = {}
+            rstd = {}
 
-                fa = workb.tile([P, D], F32, tag="fa")
-                fb = workb.tile([P, D], F32, tag="fb")
-                sa2 = workb.tile([P, D], F32, tag="sa2")
-                sb2 = workb.tile([P, D], F32, tag="sb2")
-                nc.vector.scalar_tensor_tensor(
-                    out=fa[:], in0=h[:], scalar=1.0, in1=cr_all[i][:], op0=ALU.subtract, op1=ALU.mult
-                )
-                nc.vector.scalar_tensor_tensor(
-                    out=fb[:], in0=h[:], scalar=1.0, in1=nci_all[i][:], op0=ALU.subtract, op1=ALU.mult
-                )
-                nc.vector.tensor_tensor(out=sb2[:], in0=s[:], in1=nci_all[i][:], op=ALU.mult)
-                nc.vector.tensor_tensor(out=sa2[:], in0=s[:], in1=cr_all[i][:], op=ALU.mult)
-                sums = stat.tile([P, 2], F32, tag="sums")
-                nmu = stat.tile([P, 2], F32, tag="nmu")
-                sq = stat.tile([P, 2], F32, tag="sq")
-                var = stat.tile([P, 2], F32, tag="var")
-                rstd = stat.tile([P, 2], F32, tag="rstd")
-                nc.vector.scalar_tensor_tensor(
-                    out=sb2[:], in0=sb2[:], scalar=1.0, in1=fa[:], op0=ALU.mult, op1=ALU.subtract, accum_out=sums[:, 0:1]
-                )
-                nc.vector.scalar_tensor_tensor(
-                    out=sa2[:], in0=sa2[:], scalar=1.0, in1=fb[:], op0=ALU.mult, op1=ALU.add, accum_out=sums[:, 1:2]
-                )
-                nc.vector.tensor_scalar(out=nmu[:], in0=sums[:], scalar1=-1.0 / D, scalar2=None, op0=ALU.mult)
-                nc.scalar.activation(
-                    out=h[:], in_=sb2[:], func=ACT.Square, bias=nmu[:, 0:1], scale=1.0, accum_out=sq[:, 0:1]
-                )
-                nc.scalar.activation(
-                    out=h[:], in_=sa2[:], func=ACT.Square, bias=nmu[:, 1:2], scale=1.0, accum_out=sq[:, 1:2]
-                )
-                nc.gpsimd.tensor_scalar(out=var[:], in0=sq[:], scalar1=1.0 / D, scalar2=EPS, op0=ALU.mult, op1=ALU.add)
-                nc.gpsimd.tensor_tensor(out=rstd[:], in0=var[:], in1=neghalf[:], op=ALU.pow)
-                nc.vector.scalar_tensor_tensor(
-                    out=fa[:], in0=sb2[:], scalar=nmu[:, 0:1], in1=wps[:], op0=ALU.add, op1=ALU.mult
-                )
-                nc.vector.scalar_tensor_tensor(
-                    out=fa[:], in0=fa[:], scalar=rstd[:, 0:1], in1=bps[:], op0=ALU.mult, op1=ALU.add
-                )
-                nc.sync.dma_start(out=o0_d[i], in_=fa[:])
-                nc.vector.scalar_tensor_tensor(
-                    out=fb[:], in0=sa2[:], scalar=nmu[:, 1:2], in1=wps[:], op0=ALU.add, op1=ALU.mult
-                )
-                nc.vector.scalar_tensor_tensor(
-                    out=fb[:], in0=fb[:], scalar=rstd[:, 1:2], in1=bps[:], op0=ALU.mult, op1=ALU.add
-                )
-                nc.sync.dma_start(out=o1_d[i], in_=fb[:])
+            def valid(i):
+                return 0 <= i < NT
+
+            for k in range(-3, NT + 1):
+                i = k + 3
+                if valid(i):
+                    p0[i] = [ppsum.tile([P, HALF], F32, name="p0_%d" % n, tag="p0_%d" % n) for n in range(2)]
+                    for n in range(2):
+                        for g in range(2):
+                            nc.tensor.matmul_mx(
+                                out=p0[i][n][:],
+                                lhsT=xcodes[:, i, g * P : (g + 1) * P].bitcast(FP8X4),
+                                lhsT_scale=xscales[:, i, g * P : (g + 1) * P],
+                                rhs=pcodes[:, g, n * HALF : (n + 1) * HALF].bitcast(FP8X4),
+                                rhs_scale=pscales[:, g, n * HALF : (n + 1) * HALF],
+                                start=(g == 0),
+                                stop=(g == 1),
+                            )
+                i = k
+                if valid(i):
+                    fa[i] = workb.tile([P, D], F32, name="fa", tag="fa")
+                    fb[i] = workb.tile([P, D], F32, name="fb", tag="fb")
+                    nc.vector.scalar_tensor_tensor(
+                        out=fa[i][:], in0=hh[i][:], scalar=1.0, in1=cr_all[i][:], op0=ALU.subtract, op1=ALU.mult
+                    )
+                    nc.vector.scalar_tensor_tensor(
+                        out=fb[i][:], in0=hh[i][:], scalar=1.0, in1=nci_all[i][:], op0=ALU.subtract, op1=ALU.mult
+                    )
+                    sums[i] = stat.tile([P, 2], F32, name="sums", tag="sums")
+                    nc.vector.scalar_tensor_tensor(
+                        out=sb2[i][:], in0=sb2[i][:], scalar=1.0, in1=fa[i][:], op0=ALU.mult, op1=ALU.subtract,
+                        accum_out=sums[i][:, 0:1],
+                    )
+                    nc.vector.scalar_tensor_tensor(
+                        out=sa2[i][:], in0=sa2[i][:], scalar=1.0, in1=fb[i][:], op0=ALU.mult, op1=ALU.add,
+                        accum_out=sums[i][:, 1:2],
+                    )
+                    nmu[i] = stat.tile([P, 2], F32, name="nmu", tag="nmu")
+                    nc.gpsimd.tensor_scalar(
+                        out=nmu[i][:], in0=sums[i][:], scalar1=-1.0 / D, scalar2=0.0, op0=ALU.mult, op1=ALU.add
+                    )
+                i = k + 1
+                if valid(i):
+                    hh[i] = workb.tile([P, D], F32, name="hh", tag="hh")
+                    nc.scalar.activation(out=hh[i][:], in_=vs[i][:], func=ACT.Sin, scale=math.pi)
+                    nc.scalar.activation(out=vs[i][:], in_=vs[i][:], func=ACT.Sin, scale=2.0 * math.pi)
+                    nc.scalar.activation(out=hh[i][:], in_=hh[i][:], func=ACT.Square, scale=math.sqrt(2.0))
+                i = k
+                if valid(i):
+                    sq[i] = stat.tile([P, 2], F32, name="sq", tag="sq")
+                    nc.scalar.activation(
+                        out=hh[i][:], in_=sb2[i][:], func=ACT.Square, bias=nmu[i][:, 0:1], scale=1.0,
+                        accum_out=sq[i][:, 0:1],
+                    )
+                    nc.scalar.activation(
+                        out=hh[i][:], in_=sa2[i][:], func=ACT.Square, bias=nmu[i][:, 1:2], scale=1.0,
+                        accum_out=sq[i][:, 1:2],
+                    )
+                i = k - 1
+                if valid(i):
+                    nc.vector.scalar_tensor_tensor(
+                        out=fa[i][:], in0=sb2[i][:], scalar=nmu[i][:, 0:1], in1=wps[:], op0=ALU.add, op1=ALU.mult
+                    )
+                    nc.vector.scalar_tensor_tensor(
+                        out=fa[i][:], in0=fa[i][:], scalar=rstd[i][:, 0:1], in1=bps[:], op0=ALU.mult, op1=ALU.add
+                    )
+                    nc.sync.dma_start(out=o0_d[i], in_=fa[i][:])
+                    nc.vector.scalar_tensor_tensor(
+                        out=fb[i][:], in0=sa2[i][:], scalar=nmu[i][:, 1:2], in1=wps[:], op0=ALU.add, op1=ALU.mult
+                    )
+                    nc.vector.scalar_tensor_tensor(
+                        out=fb[i][:], in0=fb[i][:], scalar=rstd[i][:, 1:2], in1=bps[:], op0=ALU.mult, op1=ALU.add
+                    )
+                    nc.sync.dma_start(out=o1_d[i], in_=fb[i][:])
+                i = k + 1
+                if valid(i):
+                    sa2[i] = workb.tile([P, D], F32, name="sa2", tag="sa2", bufs=3)
+                    nc.gpsimd.tensor_tensor(out=sa2[i][:], in0=vs[i][:], in1=cr_all[i][:], op=ALU.mult)
+                i = k
+                if valid(i):
+                    var = stat.tile([P, 2], F32, name="var", tag="var")
+                    rstd[i] = stat.tile([P, 2], F32, name="rstd", tag="rstd")
+                    nc.gpsimd.tensor_scalar(
+                        out=var[:], in0=sq[i][:], scalar1=1.0 / D, scalar2=EPS, op0=ALU.mult, op1=ALU.add
+                    )
+                    nc.gpsimd.tensor_tensor(out=rstd[i][:], in0=var[:], in1=neghalf[:], op=ALU.pow)
+                i = k + 1
+                if valid(i):
+                    sb2[i] = workb.tile([P, D], F32, name="sb2", tag="sb2", bufs=3)
+                    nc.gpsimd.tensor_tensor(out=sb2[i][:], in0=vs[i][:], in1=nci_all[i][:], op=ALU.mult)
+                i = k + 2
+                if valid(i):
+                    g_i = gp[:, i : i + 1]
+                    ki = workb.tile([P, D], I32, name="ki", tag="ki", bufs=1)
+                    vs[i] = workb.tile([P, D], F32, name="vs", tag="vs")
+                    for n in range(2):
+                        cols = slice(n * HALF, (n + 1) * HALF)
+                        nc.vector.tensor_scalar(
+                            out=ki[:, cols], in0=p0[i][n][:], scalar1=g_i, scalar2=None, op0=ALU.mult
+                        )
+                    for n in range(2):
+                        cols = slice(n * HALF, (n + 1) * HALF)
+                        nc.vector.scalar_tensor_tensor(
+                            out=vs[i][:, cols], in0=p0[i][n][:], scalar=g_i, in1=ki[:, cols], op0=ALU.mult,
+                            op1=ALU.subtract,
+                        )

@@ -33,7 +33,10 @@ def tile_quantumcoherencelayer_kernel(
 
     with ExitStack() as ctx:
         keep = ctx.enter_context(tc.tile_pool(name="keep", bufs=1))
+        work = ctx.enter_context(tc.tile_pool(name="work", bufs=1))
+        stat = ctx.enter_context(tc.tile_pool(name="stat", bufs=4))
         cpsum = ctx.enter_context(tc.psum_pool(name="cpsum", bufs=1))
+        psum = ctx.enter_context(tc.psum_pool(name="psum", bufs=1))
 
         ident = keep.tile([P, P], F32)
         make_identity(nc, ident[:])
@@ -41,6 +44,8 @@ def tile_quantumcoherencelayer_kernel(
         nc.vector.memset(eps_t[:], EPS)
         neghalf = keep.tile([P, 2], F32)
         nc.vector.memset(neghalf[:], -0.5)
+        ones = keep.tile([P, P], BF16)
+        nc.vector.memset(ones[:], 1.0)
 
         cfb = keep.tile([P, 1], BF16)
         with nc.allow_non_contiguous_dma(reason="one bfloat16 scalar to every partition"):
@@ -56,229 +61,325 @@ def tile_quantumcoherencelayer_kernel(
         ss = keep.tile([P, NT], F32)
         gp = keep.tile([P, NT], F32)
         cr_all = [keep.tile([P, D], F32, name="cr%d" % i) for i in range(NT)]
-        nci_all = [keep.tile([P, D], F32, name="nci%d" % i) for i in range(NT)]
+        nci_all = [keep.tile([P, D], F32, name="nci%d" % i, align_bytes=64) for i in range(NT)]
 
         wps = cpsum.tile([P, D], BF16)
         bps = cpsum.tile([P, D], BF16)
+        rows = nci_all[NT - 5][:].bitcast(BF16)
+        nc.vector.memset(rows, 0.0)
+        nc.scalar.dma_start(out=rows[0:1, 0:D], in_=ln_weight.rearrange("(o d) -> o d", o=1))
+        nc.scalar.dma_start(out=rows[0:1, D : 2 * D], in_=ln_bias.rearrange("(o d) -> o d", o=1))
+        for h in range(2):
+            nc.tensor.matmul(
+                out=wps[:, h * HALF : (h + 1) * HALF], lhsT=ones[:], rhs=rows[:, h * HALF : (h + 1) * HALF],
+                start=True, stop=True,
+            )
+        for h in range(2):
+            nc.tensor.matmul(
+                out=bps[:, h * HALF : (h + 1) * HALF], lhsT=ones[:], rhs=rows[:, D + h * HALF : D + (h + 1) * HALF],
+                start=True, stop=True,
+            )
 
-        with tc.tile_pool(name="stage", bufs=1) as stage, tc.tile_pool(name="xin", bufs=3) as xin, tc.tile_pool(
-            name="worka", bufs=2
-        ) as worka, tc.psum_pool(name="tpsum", bufs=2) as tpsum:
-            rows = stage.tile([P, 2 * D], BF16)
-            nc.vector.memset(rows[:], 0.0)
-            nc.scalar.dma_start(out=rows[0:1, 0:D], in_=ln_weight.rearrange("(o d) -> o d", o=1))
-            nc.scalar.dma_start(out=rows[0:1, D : 2 * D], in_=ln_bias.rearrange("(o d) -> o d", o=1))
-            ones = stage.tile([P, P], BF16)
-            nc.vector.memset(ones[:], 1.0)
-            for h in range(2):
-                nc.tensor.matmul(
-                    out=wps[:, h * HALF : (h + 1) * HALF],
-                    lhsT=ones[:],
-                    rhs=rows[:, h * HALF : (h + 1) * HALF],
-                    start=True,
-                    stop=True,
-                )
-            for h in range(2):
-                nc.tensor.matmul(
-                    out=bps[:, h * HALF : (h + 1) * HALF],
-                    lhsT=ones[:],
-                    rhs=rows[:, D + h * HALF : D + (h + 1) * HALF],
-                    start=True,
-                    stop=True,
-                )
+        x = {}
+        xt = {}
+        gt = {}
+        xps = {}
+        sa = {}
+        sb = {}
+        sr = {}
+        si = {}
+        p0 = {}
+        vs = {}
+        hh = {}
+        fa = {}
+        fb = {}
+        sa2 = {}
+        sb2 = {}
+        sums = {}
+        nmu = {}
+        sq = {}
+        rstd = {}
 
-            for i in range(NT):
-                xr = xin.tile([P, D], BF16, tag="xr")
-                nc.sync.dma_start(out=xr[:], in_=xr_d[i])
-                xi = xin.tile([P, D], BF16, tag="xi")
-                nc.sync.dma_start(out=xi[:], in_=xi_d[i])
+        def big(tag, bufs, dtype):
+            return work.tile([P, D], dtype, name=tag, tag=tag, bufs=bufs, align_bytes=64)
 
-                if i == 1:
-                    for g in range(2):
-                        raw = stage.tile([P, 4, D], BF16, tag="raw")
-                        for u in range(2):
-                            k0 = 512 * g + 256 * u
-                            nc.sync.dma_start(
-                                out=raw[:, 2 * u : 2 * u + 2, :],
-                                in_=phase_matrix[k0 : k0 + 256, :].rearrange("(q e) c -> q e c", e=2),
-                            )
-                        pg = stage.tile([P, D, 4], BF16, tag="pg", align_bytes=64)
-                        nc.vector.tensor_copy(
-                            out=pg[:].rearrange("p (c i) t -> p c t i", i=4),
-                            in_=raw[:].rearrange("p t (c i) -> p c t i", i=4),
-                        )
-                        nc.vector.quantize_mx(
-                            out=pcodes[:, g, :].bitcast(FP8X4),
-                            scales=pscales[:, g, :],
-                            in_=pg[:].rearrange("p c t -> p (c t)"),
-                        )
+        def bank(b):
+            return psum.tile([P, HALF], F32, name="b%d" % b, tag="b%d" % b)
 
-                xt = tpsum.tile([P, 4 * P], F32, tag="xt")
-                xw = xr[:].bitcast(F32)
+        def load(i):
+            x[i] = work.tile([P, 2, D], BF16, name="x", tag="x", bufs=3, align_bytes=64)
+            nc.sync.dma_start(out=x[i][:, 0, :], in_=xr_d[i])
+            nc.sync.dma_start(out=x[i][:, 1, :], in_=xi_d[i])
+
+        def p_raw(c):
+            return cr_all[NT - 4 + c][:].bitcast(BF16).rearrange("p (t c) -> p t c", t=4)
+
+        def p_load():
+            for c in range(4):
+                g, hf = divmod(c, 2)
+                for u in range(2):
+                    k0 = 512 * g + 256 * u
+                    nc.sync.dma_start(
+                        out=p_raw(c)[:, 2 * u : 2 * u + 2, :],
+                        in_=phase_matrix[k0 : k0 + 256, hf * HALF : (hf + 1) * HALF].rearrange("(q e) c -> q e c", e=2),
+                    )
+
+        def p_quantise(c):
+            g, hf = divmod(c, 2)
+            pg = nci_all[NT - 4 + c][:].bitcast(BF16)
+            nc.vector.tensor_copy(
+                out=pg.rearrange("p (c i t) -> p c t i", i=4, t=4), in_=p_raw(c).rearrange("p t (c i) -> p c t i", i=4)
+            )
+            nc.vector.quantize_mx(
+                out=pcodes[:, g, hf * HALF : (hf + 1) * HALF].bitcast(FP8X4),
+                scales=pscales[:, g, hf * HALF : (hf + 1) * HALF],
+                in_=pg,
+            )
+
+        def squares(i):
+            sa[i] = big("sa", 3, F32)
+            sb[i] = big("sb", 2, F32)
+            sr[i] = big("sr", 3, F32)
+            si[i] = big("si", 2, F32)
+            nc.scalar.activation(out=sa[i][:], in_=x[i][:, 0, :], func=ACT.Square, bias=eps_t[:, 0:1], scale=1.0)
+            nc.scalar.activation(out=sb[i][:], in_=x[i][:, 1, :], func=ACT.Square, bias=eps_t[:, 0:1], scale=1.0)
+            nc.scalar.activation(out=sr[i][:], in_=x[i][:, 0, :], func=ACT.Square)
+            nc.scalar.activation(out=si[i][:], in_=x[i][:, 1, :], func=ACT.Square)
+
+        def transpose_there(i):
+            xt[i] = [bank(0), bank(1)]
+            for c in range(2):
+                xw = x[i][:, c, :].bitcast(F32)
                 for j in range(4):
-                    nc.tensor.transpose(out=xt[:, j * P : (j + 1) * P], in_=xw[:, j * P : (j + 1) * P], identity=ident[:])
-                grouped = worka.tile([P, 2, P, 4], BF16, tag="grouped", align_bytes=64)
-                nc.scalar.copy(
-                    out=grouped[:].bitcast(F32),
-                    in_=xt[:].rearrange("p (g u r) -> p g r u", g=2, u=2),
-                )
+                    nc.tensor.transpose(
+                        out=xt[i][c][:, j * P : (j + 1) * P], in_=xw[:, j * P : (j + 1) * P], identity=ident[:]
+                    )
 
-                sa = worka.tile([P, D], F32, tag="sa")
-                sb = worka.tile([P, D], F32, tag="sb")
-                sr = worka.tile([P, D], F32, tag="sr")
-                si = worka.tile([P, D], F32, tag="si")
-                nc.scalar.activation(out=sa[:], in_=xr[:], func=ACT.Square, bias=eps_t[:, 0:1], scale=1.0)
-                nc.scalar.activation(out=sb[:], in_=xi[:], func=ACT.Square, bias=eps_t[:, 0:1], scale=1.0)
-                nc.scalar.activation(out=sr[:], in_=xr[:], func=ACT.Square)
-                nc.scalar.activation(out=si[:], in_=xi[:], func=ACT.Square)
-                nc.vector.tensor_tensor(out=sa[:], in0=sa[:], in1=sb[:], op=ALU.add)
-                nc.vector.tensor_tensor(out=sr[:], in0=sr[:], in1=si[:], op=ALU.add)
-                nc.vector.quantize_mx(
-                    out=xcodes[:, i, :].bitcast(FP8X4),
-                    scales=xscales[:, i, :],
-                    in_=grouped[:].rearrange("p g r t -> p (g r t)"),
-                )
-                nc.scalar.activation(out=sa[:], in_=sa[:], func=ACT.Abs_reciprocal_sqrt)
-                nc.scalar.activation(out=sr[:], in_=sr[:], func=ACT.Abs_reciprocal_sqrt, bias=eps_t[:, 0:1], scale=1.0)
-                nc.vector.scalar_tensor_tensor(
-                    out=sb[:], in0=xr[:], scalar=EPS, in1=sa[:], op0=ALU.add, op1=ALU.mult, accum_out=sc[:, i : i + 1]
-                )
-                nc.vector.scalar_tensor_tensor(
-                    out=si[:], in0=xi[:], scalar=EPS, in1=sa[:], op0=ALU.add, op1=ALU.mult, accum_out=ss[:, i : i + 1]
-                )
-                nc.vector.tensor_tensor(out=cr_all[i][:], in0=xr[:], in1=sr[:], op=ALU.mult)
-                nc.vector.scalar_tensor_tensor(
-                    out=nci_all[i][:], in0=xi[:], scalar=-1.0, in1=sr[:], op0=ALU.mult, op1=ALU.mult
-                )
+        def add_squares(i):
+            nc.gpsimd.tensor_tensor(out=sa[i][:], in0=sa[i][:], in1=sb[i][:], op=ALU.add)
+            nc.gpsimd.tensor_tensor(out=sr[i][:], in0=sr[i][:], in1=si[i][:], op=ALU.add)
 
-            nc.vector.tensor_tensor(out=sc[:], in0=sc[:], in1=sc[:], op=ALU.mult)
-            nc.vector.tensor_tensor(out=ss[:], in0=ss[:], in1=ss[:], op=ALU.mult)
-            nc.vector.tensor_tensor(out=sc[:], in0=sc[:], in1=ss[:], op=ALU.add)
-            nc.vector.tensor_scalar(
-                out=sc[:], in0=sc[:], scalar1=-1.0 / (D * D), scalar2=1.0, op0=ALU.mult, op1=ALU.add
+        def evacuate(i):
+            gt[i] = work.tile([P, 2, HALF], F32, name="g", tag="g", bufs=2, align_bytes=64)
+            nc.vector.tensor_copy(
+                out=gt[i][:, 0, :].rearrange("p (g r u) -> p g r u", g=2, u=2),
+                in_=xt[i][0][:].rearrange("p (g u r) -> p g r u", g=2, u=2),
             )
-            nc.vector.tensor_scalar(
-                out=gp[:], in0=sc[:], scalar1=cf32[:, 0:1], scalar2=1.0 / (2.0 * math.pi), op0=ALU.mult, op1=ALU.mult
+            nc.vector.tensor_copy(out=gt[i][:, 1, :], in_=xt[i][1][:])
+
+        def quantise(i):
+            nc.vector.quantize_mx(
+                out=xcodes[:, i, :].bitcast(FP8X4), scales=xscales[:, i, :], in_=gt[i][:, 0, :].bitcast(BF16)
             )
 
-        with tc.tile_pool(name="workb", bufs=2) as workb, tc.tile_pool(name="stat", bufs=4) as stat, tc.psum_pool(
-            name="ppsum", bufs=2
-        ) as ppsum, tc.manual_schedule():
-            p0 = {}
-            vs = {}
-            hh = {}
-            fa = {}
-            fb = {}
-            sa2 = {}
-            sb2 = {}
-            sums = {}
-            nmu = {}
-            sq = {}
-            rstd = {}
+        def transpose_back(i):
+            b = 2 + 2 * (i % 2)
+            xps[i] = [bank(b), bank(b + 1)]
+            gw = gt[i][:, 0, :].rearrange("p (g r u) -> p g r u", g=2, u=2)
+            for g in range(2):
+                for u in range(2):
+                    j = 2 * g + u
+                    nc.tensor.transpose(out=xps[i][0][:, j * P : (j + 1) * P], in_=gw[:, g, :, u], identity=ident[:])
+            for j in range(4):
+                nc.tensor.transpose(
+                    out=xps[i][1][:, j * P : (j + 1) * P], in_=gt[i][:, 1, j * P : (j + 1) * P], identity=ident[:]
+                )
 
-            def valid(i):
-                return 0 <= i < NT
+        def rsqrts(i):
+            nc.scalar.activation(out=sa[i][:], in_=sa[i][:], func=ACT.Abs_reciprocal_sqrt)
+            nc.scalar.activation(
+                out=sr[i][:], in_=sr[i][:], func=ACT.Abs_reciprocal_sqrt, bias=eps_t[:, 0:1], scale=1.0
+            )
 
-            for k in range(-3, NT + 1):
-                i = k + 3
-                if valid(i):
-                    p0[i] = [ppsum.tile([P, HALF], F32, name="p0_%d" % n, tag="p0_%d" % n) for n in range(2)]
-                    for n in range(2):
-                        for g in range(2):
-                            nc.tensor.matmul_mx(
-                                out=p0[i][n][:],
-                                lhsT=xcodes[:, i, g * P : (g + 1) * P].bitcast(FP8X4),
-                                lhsT_scale=xscales[:, i, g * P : (g + 1) * P],
-                                rhs=pcodes[:, g, n * HALF : (n + 1) * HALF].bitcast(FP8X4),
-                                rhs_scale=pscales[:, g, n * HALF : (n + 1) * HALF],
-                                start=(g == 0),
-                                stop=(g == 1),
-                            )
-                i = k
-                if valid(i):
-                    fa[i] = workb.tile([P, D], F32, name="fa", tag="fa")
-                    fb[i] = workb.tile([P, D], F32, name="fb", tag="fb")
-                    nc.vector.scalar_tensor_tensor(
-                        out=fa[i][:], in0=hh[i][:], scalar=1.0, in1=cr_all[i][:], op0=ALU.subtract, op1=ALU.mult
+        def phase_sums(i):
+            junk = big("j", 1, F32)
+            nc.vector.scalar_tensor_tensor(
+                out=junk[:], in0=xps[i][0][:].bitcast(BF16), scalar=EPS, in1=sa[i][:], op0=ALU.add, op1=ALU.mult,
+                accum_out=sc[:, i : i + 1],
+            )
+            nc.vector.scalar_tensor_tensor(
+                out=junk[:], in0=xps[i][1][:].bitcast(BF16), scalar=EPS, in1=sa[i][:], op0=ALU.add, op1=ALU.mult,
+                accum_out=ss[:, i : i + 1],
+            )
+
+        def normalise(i):
+            nc.vector.tensor_tensor(out=cr_all[i][:], in0=xps[i][0][:].bitcast(BF16), in1=sr[i][:], op=ALU.mult)
+            nc.vector.scalar_tensor_tensor(
+                out=nci_all[i][:], in0=xps[i][1][:].bitcast(BF16), scalar=-1.0, in1=sr[i][:], op0=ALU.mult, op1=ALU.mult
+            )
+
+        def gains(lo, hi):
+            cols = slice(lo, hi)
+            nc.vector.tensor_tensor(out=sc[:, cols], in0=sc[:, cols], in1=sc[:, cols], op=ALU.mult)
+            nc.vector.tensor_tensor(out=ss[:, cols], in0=ss[:, cols], in1=ss[:, cols], op=ALU.mult)
+            nc.vector.tensor_tensor(out=sc[:, cols], in0=sc[:, cols], in1=ss[:, cols], op=ALU.add)
+            nc.vector.tensor_scalar(
+                out=sc[:, cols], in0=sc[:, cols], scalar1=-1.0 / (D * D), scalar2=1.0, op0=ALU.mult, op1=ALU.add
+            )
+            nc.vector.tensor_scalar(
+                out=gp[:, cols], in0=sc[:, cols], scalar1=cf32[:, 0:1], scalar2=1.0 / (2.0 * math.pi), op0=ALU.mult,
+                op1=ALU.mult,
+            )
+
+        def product(i):
+            b = 2 * (i % 3)
+            p0[i] = [bank(b), bank(b + 1)]
+            for n in range(2):
+                for g in range(2):
+                    nc.tensor.matmul_mx(
+                        out=p0[i][n][:],
+                        lhsT=xcodes[:, i, g * P : (g + 1) * P].bitcast(FP8X4),
+                        lhsT_scale=xscales[:, i, g * P : (g + 1) * P],
+                        rhs=pcodes[:, g, n * HALF : (n + 1) * HALF].bitcast(FP8X4),
+                        rhs_scale=pscales[:, g, n * HALF : (n + 1) * HALF],
+                        start=(g == 0),
+                        stop=(g == 1),
                     )
-                    nc.vector.scalar_tensor_tensor(
-                        out=fb[i][:], in0=hh[i][:], scalar=1.0, in1=nci_all[i][:], op0=ALU.subtract, op1=ALU.mult
-                    )
-                    sums[i] = stat.tile([P, 2], F32, name="sums", tag="sums")
-                    nc.vector.scalar_tensor_tensor(
-                        out=sb2[i][:], in0=sb2[i][:], scalar=1.0, in1=fa[i][:], op0=ALU.mult, op1=ALU.subtract,
-                        accum_out=sums[i][:, 0:1],
-                    )
-                    nc.vector.scalar_tensor_tensor(
-                        out=sa2[i][:], in0=sa2[i][:], scalar=1.0, in1=fb[i][:], op0=ALU.mult, op1=ALU.add,
-                        accum_out=sums[i][:, 1:2],
-                    )
-                    nmu[i] = stat.tile([P, 2], F32, name="nmu", tag="nmu")
-                    nc.gpsimd.tensor_scalar(
-                        out=nmu[i][:], in0=sums[i][:], scalar1=-1.0 / D, scalar2=0.0, op0=ALU.mult, op1=ALU.add
-                    )
-                i = k + 1
-                if valid(i):
-                    hh[i] = workb.tile([P, D], F32, name="hh", tag="hh")
-                    nc.scalar.activation(out=hh[i][:], in_=vs[i][:], func=ACT.Sin, scale=math.pi)
-                    nc.scalar.activation(out=vs[i][:], in_=vs[i][:], func=ACT.Sin, scale=2.0 * math.pi)
-                    nc.scalar.activation(out=hh[i][:], in_=hh[i][:], func=ACT.Square, scale=math.sqrt(2.0))
-                i = k
-                if valid(i):
-                    sq[i] = stat.tile([P, 2], F32, name="sq", tag="sq")
-                    nc.scalar.activation(
-                        out=hh[i][:], in_=sb2[i][:], func=ACT.Square, bias=nmu[i][:, 0:1], scale=1.0,
-                        accum_out=sq[i][:, 0:1],
-                    )
-                    nc.scalar.activation(
-                        out=hh[i][:], in_=sa2[i][:], func=ACT.Square, bias=nmu[i][:, 1:2], scale=1.0,
-                        accum_out=sq[i][:, 1:2],
-                    )
-                i = k - 1
-                if valid(i):
-                    nc.vector.scalar_tensor_tensor(
-                        out=fa[i][:], in0=sb2[i][:], scalar=nmu[i][:, 0:1], in1=wps[:], op0=ALU.add, op1=ALU.mult
-                    )
-                    nc.vector.scalar_tensor_tensor(
-                        out=fa[i][:], in0=fa[i][:], scalar=rstd[i][:, 0:1], in1=bps[:], op0=ALU.mult, op1=ALU.add
-                    )
-                    nc.sync.dma_start(out=o0_d[i], in_=fa[i][:])
-                    nc.vector.scalar_tensor_tensor(
-                        out=fb[i][:], in0=sa2[i][:], scalar=nmu[i][:, 1:2], in1=wps[:], op0=ALU.add, op1=ALU.mult
-                    )
-                    nc.vector.scalar_tensor_tensor(
-                        out=fb[i][:], in0=fb[i][:], scalar=rstd[i][:, 1:2], in1=bps[:], op0=ALU.mult, op1=ALU.add
-                    )
-                    nc.sync.dma_start(out=o1_d[i], in_=fb[i][:])
-                i = k + 1
-                if valid(i):
-                    sa2[i] = workb.tile([P, D], F32, name="sa2", tag="sa2", bufs=3)
-                    nc.gpsimd.tensor_tensor(out=sa2[i][:], in0=vs[i][:], in1=cr_all[i][:], op=ALU.mult)
-                i = k
-                if valid(i):
-                    var = stat.tile([P, 2], F32, name="var", tag="var")
-                    rstd[i] = stat.tile([P, 2], F32, name="rstd", tag="rstd")
-                    nc.gpsimd.tensor_scalar(
-                        out=var[:], in0=sq[i][:], scalar1=1.0 / D, scalar2=EPS, op0=ALU.mult, op1=ALU.add
-                    )
-                    nc.gpsimd.tensor_tensor(out=rstd[i][:], in0=var[:], in1=neghalf[:], op=ALU.pow)
-                i = k + 1
-                if valid(i):
-                    sb2[i] = workb.tile([P, D], F32, name="sb2", tag="sb2", bufs=3)
-                    nc.gpsimd.tensor_tensor(out=sb2[i][:], in0=vs[i][:], in1=nci_all[i][:], op=ALU.mult)
-                i = k + 2
-                if valid(i):
-                    g_i = gp[:, i : i + 1]
-                    ki = workb.tile([P, D], I32, name="ki", tag="ki", bufs=1)
-                    vs[i] = workb.tile([P, D], F32, name="vs", tag="vs")
-                    for n in range(2):
-                        cols = slice(n * HALF, (n + 1) * HALF)
-                        nc.vector.tensor_scalar(
-                            out=ki[:, cols], in0=p0[i][n][:], scalar1=g_i, scalar2=None, op0=ALU.mult
-                        )
-                    for n in range(2):
-                        cols = slice(n * HALF, (n + 1) * HALF)
-                        nc.vector.scalar_tensor_tensor(
-                            out=vs[i][:, cols], in0=p0[i][n][:], scalar=g_i, in1=ki[:, cols], op0=ALU.mult,
-                            op1=ALU.subtract,
-                        )
+
+        def reduce_range(i):
+            g_i = gp[:, i : i + 1]
+            ki = big("j", 1, I32)
+            vs[i] = big("x", 3, F32)
+            for n in range(2):
+                cols = slice(n * HALF, (n + 1) * HALF)
+                nc.vector.tensor_scalar(out=ki[:, cols], in0=p0[i][n][:], scalar1=g_i, scalar2=None, op0=ALU.mult)
+            for n in range(2):
+                cols = slice(n * HALF, (n + 1) * HALF)
+                nc.vector.scalar_tensor_tensor(
+                    out=vs[i][:, cols], in0=p0[i][n][:], scalar=g_i, in1=ki[:, cols], op0=ALU.mult, op1=ALU.subtract
+                )
+
+        def sines(i):
+            hh[i] = big("g", 2, F32)
+            nc.scalar.activation(out=hh[i][:], in_=vs[i][:], func=ACT.Sin, scale=math.pi)
+            nc.scalar.activation(out=vs[i][:], in_=vs[i][:], func=ACT.Sin, scale=2.0 * math.pi)
+            nc.scalar.activation(out=hh[i][:], in_=hh[i][:], func=ACT.Square, scale=math.sqrt(2.0))
+
+        def sine_product_a(i):
+            sa2[i] = big("sa", 3, F32)
+            nc.gpsimd.tensor_tensor(out=sa2[i][:], in0=vs[i][:], in1=cr_all[i][:], op=ALU.mult)
+
+        def sine_product_b(i):
+            sb2[i] = big("sr", 3, F32)
+            nc.gpsimd.tensor_tensor(out=sb2[i][:], in0=vs[i][:], in1=nci_all[i][:], op=ALU.mult)
+
+        def rotate(i):
+            fa[i] = big("sb", 2, F32)
+            fb[i] = big("si", 2, F32)
+            nc.vector.scalar_tensor_tensor(
+                out=fa[i][:], in0=hh[i][:], scalar=1.0, in1=cr_all[i][:], op0=ALU.subtract, op1=ALU.mult
+            )
+            nc.vector.scalar_tensor_tensor(
+                out=fb[i][:], in0=hh[i][:], scalar=1.0, in1=nci_all[i][:], op0=ALU.subtract, op1=ALU.mult
+            )
+            sums[i] = stat.tile([P, 2], F32, name="sums", tag="sums")
+            nc.vector.scalar_tensor_tensor(
+                out=sb2[i][:], in0=sb2[i][:], scalar=1.0, in1=fa[i][:], op0=ALU.mult, op1=ALU.subtract,
+                accum_out=sums[i][:, 0:1],
+            )
+            nc.vector.scalar_tensor_tensor(
+                out=sa2[i][:], in0=sa2[i][:], scalar=1.0, in1=fb[i][:], op0=ALU.mult, op1=ALU.add,
+                accum_out=sums[i][:, 1:2],
+            )
+
+        def minus_means(i):
+            nmu[i] = stat.tile([P, 2], F32, name="nmu", tag="nmu")
+            nc.gpsimd.tensor_scalar(
+                out=nmu[i][:], in0=sums[i][:], scalar1=-1.0 / D, scalar2=0.0, op0=ALU.mult, op1=ALU.add
+            )
+
+        def squared_deviations(i):
+            sq[i] = stat.tile([P, 2], F32, name="sq", tag="sq")
+            nc.scalar.activation(
+                out=hh[i][:], in_=sb2[i][:], func=ACT.Square, bias=nmu[i][:, 0:1], scale=1.0, accum_out=sq[i][:, 0:1]
+            )
+            nc.scalar.activation(
+                out=hh[i][:], in_=sa2[i][:], func=ACT.Square, bias=nmu[i][:, 1:2], scale=1.0, accum_out=sq[i][:, 1:2]
+            )
+
+        def inverse_deviations(i):
+            var = stat.tile([P, 2], F32, name="var", tag="var")
+            rstd[i] = stat.tile([P, 2], F32, name="rstd", tag="rstd")
+            nc.gpsimd.tensor_scalar(out=var[:], in0=sq[i][:], scalar1=1.0 / D, scalar2=EPS, op0=ALU.mult, op1=ALU.add)
+            nc.gpsimd.tensor_tensor(out=rstd[i][:], in0=var[:], in1=neghalf[:], op=ALU.pow)
+
+        def scale_shift_store(i):
+            nc.vector.scalar_tensor_tensor(
+                out=fa[i][:], in0=sb2[i][:], scalar=nmu[i][:, 0:1], in1=wps[:], op0=ALU.add, op1=ALU.mult
+            )
+            nc.vector.scalar_tensor_tensor(
+                out=fa[i][:], in0=fa[i][:], scalar=rstd[i][:, 0:1], in1=bps[:], op0=ALU.mult, op1=ALU.add
+            )
+            nc.sync.dma_start(out=o0_d[i], in_=fa[i][:])
+            nc.vector.scalar_tensor_tensor(
+                out=fb[i][:], in0=sa2[i][:], scalar=nmu[i][:, 1:2], in1=wps[:], op0=ALU.add, op1=ALU.mult
+            )
+            nc.vector.scalar_tensor_tensor(
+                out=fb[i][:], in0=fb[i][:], scalar=rstd[i][:, 1:2], in1=bps[:], op0=ALU.mult, op1=ALU.add
+            )
+            nc.sync.dma_start(out=o1_d[i], in_=fb[i][:])
+
+        def ok(i):
+            return 0 <= i < NT
+
+        with tc.manual_schedule():
+            for k in range(-2, NT + 1):
+                if ok(k + 2):
+                    load(k + 2)
+                if k == 0:
+                    p_load()
+                if ok(k + 1):
+                    squares(k + 1)
+                    transpose_there(k + 1)
+                    add_squares(k + 1)
+                if k == NT - 1:
+                    product(0)
+                    reduce_range(0)
+                if k == NT:
+                    product(1)
+                    reduce_range(1)
+                if ok(k - 1):
+                    phase_sums(k - 1)
+                if ok(k):
+                    quantise(k)
+                if ok(k - 1):
+                    normalise(k - 1)
+                if ok(k + 1):
+                    evacuate(k + 1)
+                if 1 <= k <= 4:
+                    p_quantise(k - 1)
+                if k == NT // 2:
+                    gains(0, NT // 2)
+                if ok(k):
+                    transpose_back(k)
+                    rsqrts(k)
+            gains(NT // 2, NT)
+            sines(0)
+            sine_product_a(0)
+            sine_product_b(0)
+            sines(1)
+            sine_product_a(1)
+            product(2)
+            reduce_range(2)
+            for k in range(0, NT + 1):
+                if ok(k + 3):
+                    product(k + 3)
+                if ok(k):
+                    rotate(k)
+                    minus_means(k)
+                if k >= 1 and ok(k + 1):
+                    sines(k + 1)
+                if ok(k):
+                    squared_deviations(k)
+                if ok(k - 1):
+                    scale_shift_store(k - 1)
+                if k >= 1 and ok(k + 1):
+                    sine_product_a(k + 1)
+                if k == 0:
+                    sine_product_b(1)
+                if ok(k):
+                    inverse_deviations(k)
+                if k >= 1 and ok(k + 1):
+                    sine_product_b(k + 1)
+                if ok(k + 3):
+                    reduce_range(k + 3)

@@ -33,10 +33,7 @@ def tile_quantumcoherencelayer_kernel(
 
     with ExitStack() as ctx:
         keep = ctx.enter_context(tc.tile_pool(name="keep", bufs=1))
-        work = ctx.enter_context(tc.tile_pool(name="work", bufs=1))
-        stat = ctx.enter_context(tc.tile_pool(name="stat", bufs=4))
         cpsum = ctx.enter_context(tc.psum_pool(name="cpsum", bufs=1))
-        psum = ctx.enter_context(tc.psum_pool(name="psum", bufs=1))
 
         ident = keep.tile([P, P], F32)
         make_identity(nc, ident[:])
@@ -44,8 +41,6 @@ def tile_quantumcoherencelayer_kernel(
         nc.vector.memset(eps_t[:], EPS)
         neghalf = keep.tile([P, 2], F32)
         nc.vector.memset(neghalf[:], -0.5)
-        ones = keep.tile([P, P], BF16)
-        nc.vector.memset(ones[:], 1.0)
 
         cfb = keep.tile([P, 1], BF16)
         with nc.allow_non_contiguous_dma(reason="one bfloat16 scalar to every partition"):
@@ -60,326 +55,273 @@ def tile_quantumcoherencelayer_kernel(
         sc = keep.tile([P, NT], F32)
         ss = keep.tile([P, NT], F32)
         gp = keep.tile([P, NT], F32)
+        wbt = keep.tile([P, 16], F32)
         cr_all = [keep.tile([P, D], F32, name="cr%d" % i) for i in range(NT)]
-        nci_all = [keep.tile([P, D], F32, name="nci%d" % i, align_bytes=64) for i in range(NT)]
+        nci_all = [keep.tile([P, D], F32, name="nci%d" % i) for i in range(NT)]
 
         wps = cpsum.tile([P, D], BF16)
         bps = cpsum.tile([P, D], BF16)
-        rows = nci_all[NT - 5][:].bitcast(BF16)
-        nc.vector.memset(rows, 0.0)
-        nc.scalar.dma_start(out=rows[0:1, 0:D], in_=ln_weight.rearrange("(o d) -> o d", o=1))
-        nc.scalar.dma_start(out=rows[0:1, D : 2 * D], in_=ln_bias.rearrange("(o d) -> o d", o=1))
-        for h in range(2):
-            nc.tensor.matmul(
-                out=wps[:, h * HALF : (h + 1) * HALF], lhsT=ones[:], rhs=rows[:, h * HALF : (h + 1) * HALF],
-                start=True, stop=True,
-            )
-        for h in range(2):
-            nc.tensor.matmul(
-                out=bps[:, h * HALF : (h + 1) * HALF], lhsT=ones[:], rhs=rows[:, D + h * HALF : D + (h + 1) * HALF],
-                start=True, stop=True,
-            )
 
-        x = {}
-        xt = {}
-        gt = {}
-        xps = {}
-        sa = {}
-        sb = {}
-        sr = {}
-        si = {}
-        p0 = {}
-        vs = {}
-        hh = {}
-        fa = {}
-        fb = {}
-        sa2 = {}
-        sb2 = {}
-        sums = {}
-        nmu = {}
-        sq = {}
-        rstd = {}
+        with tc.tile_pool(name="stage", bufs=1) as stage, tc.tile_pool(name="xin", bufs=3) as xin, tc.tile_pool(
+            name="worka", bufs=2
+        ) as worka, tc.psum_pool(name="tpsum", bufs=2) as tpsum:
+            rows = stage.tile([P, 2 * D], BF16)
+            nc.vector.memset(rows[:], 0.0)
+            nc.scalar.dma_start(out=rows[0:1, 0:D], in_=ln_weight.rearrange("(o d) -> o d", o=1))
+            nc.scalar.dma_start(out=rows[0:1, D : 2 * D], in_=ln_bias.rearrange("(o d) -> o d", o=1))
+            ones = stage.tile([P, P], BF16)
+            nc.vector.memset(ones[:], 1.0)
+            for h in range(2):
+                nc.tensor.matmul(
+                    out=wps[:, h * HALF : (h + 1) * HALF],
+                    lhsT=ones[:],
+                    rhs=rows[:, h * HALF : (h + 1) * HALF],
+                    start=True,
+                    stop=True,
+                )
+            for h in range(2):
+                nc.tensor.matmul(
+                    out=bps[:, h * HALF : (h + 1) * HALF],
+                    lhsT=ones[:],
+                    rhs=rows[:, D + h * HALF : D + (h + 1) * HALF],
+                    start=True,
+                    stop=True,
+                )
 
-        def big(tag, bufs, dtype):
-            return work.tile([P, D], dtype, name=tag, tag=tag, bufs=bufs, align_bytes=64)
+            wb = stage.tile([P, P], BF16)
+            nc.vector.memset(wb[:], 0.0)
+            nc.scalar.dma_start(out=wb[0:8, :], in_=ln_weight.rearrange("(j p) -> j p", p=P))
+            nc.scalar.dma_start(out=wb[8:16, :], in_=ln_bias.rearrange("(j p) -> j p", p=P))
+            wb32 = stage.tile([P, P], F32)
+            nc.vector.tensor_copy(out=wb32[:], in_=wb[:])
+            wbt_ps = tpsum.tile([P, 4 * P], F32, tag="xt")
+            nc.tensor.transpose(out=wbt_ps[:, 0:P], in_=wb32[:], identity=ident[:])
+            nc.vector.tensor_copy(out=wbt[:], in_=wbt_ps[:, 0:16])
 
-        def bank(b):
-            return psum.tile([P, HALF], F32, name="b%d" % b, tag="b%d" % b)
+            for i in range(NT):
+                xr = xin.tile([P, D], BF16, tag="xr")
+                nc.sync.dma_start(out=xr[:], in_=xr_d[i])
+                xi = xin.tile([P, D], BF16, tag="xi")
+                nc.sync.dma_start(out=xi[:], in_=xi_d[i])
 
-        def load(i):
-            x[i] = work.tile([P, 2, D], BF16, name="x", tag="x", bufs=3, align_bytes=64)
-            nc.sync.dma_start(out=x[i][:, 0, :], in_=xr_d[i])
-            nc.sync.dma_start(out=x[i][:, 1, :], in_=xi_d[i])
+                if i == 1:
+                    for g in range(2):
+                        raw = stage.tile([P, 4, D], BF16, tag="raw")
+                        for u in range(2):
+                            k0 = 512 * g + 256 * u
+                            nc.sync.dma_start(
+                                out=raw[:, 2 * u : 2 * u + 2, :],
+                                in_=phase_matrix[k0 : k0 + 256, :].rearrange("(q e) c -> q e c", e=2),
+                            )
+                        pg = stage.tile([P, D, 4], BF16, tag="pg", align_bytes=64)
+                        nc.vector.tensor_copy(
+                            out=pg[:].rearrange("p (c i) t -> p c t i", i=4),
+                            in_=raw[:].rearrange("p t (c i) -> p c t i", i=4),
+                        )
+                        nc.vector.quantize_mx(
+                            out=pcodes[:, g, :].bitcast(FP8X4),
+                            scales=pscales[:, g, :],
+                            in_=pg[:].rearrange("p c t -> p (c t)"),
+                        )
 
-        def p_raw(c):
-            return cr_all[NT - 4 + c][:].bitcast(BF16).rearrange("p (t c) -> p t c", t=4)
-
-        def p_load():
-            for c in range(4):
-                g, hf = divmod(c, 2)
-                for u in range(2):
-                    k0 = 512 * g + 256 * u
-                    nc.sync.dma_start(
-                        out=p_raw(c)[:, 2 * u : 2 * u + 2, :],
-                        in_=phase_matrix[k0 : k0 + 256, hf * HALF : (hf + 1) * HALF].rearrange("(q e) c -> q e c", e=2),
-                    )
-
-        def p_quantise(c):
-            g, hf = divmod(c, 2)
-            pg = nci_all[NT - 4 + c][:].bitcast(BF16)
-            nc.vector.tensor_copy(
-                out=pg.rearrange("p (c i t) -> p c t i", i=4, t=4), in_=p_raw(c).rearrange("p t (c i) -> p c t i", i=4)
-            )
-            nc.vector.quantize_mx(
-                out=pcodes[:, g, hf * HALF : (hf + 1) * HALF].bitcast(FP8X4),
-                scales=pscales[:, g, hf * HALF : (hf + 1) * HALF],
-                in_=pg,
-            )
-
-        def squares(i):
-            sa[i] = big("sa", 3, F32)
-            sb[i] = big("sb", 2, F32)
-            sr[i] = big("sr", 3, F32)
-            si[i] = big("si", 2, F32)
-            nc.scalar.activation(out=sa[i][:], in_=x[i][:, 0, :], func=ACT.Square, bias=eps_t[:, 0:1], scale=1.0)
-            nc.scalar.activation(out=sb[i][:], in_=x[i][:, 1, :], func=ACT.Square, bias=eps_t[:, 0:1], scale=1.0)
-            nc.scalar.activation(out=sr[i][:], in_=x[i][:, 0, :], func=ACT.Square)
-            nc.scalar.activation(out=si[i][:], in_=x[i][:, 1, :], func=ACT.Square)
-
-        def transpose_there(i):
-            xt[i] = [bank(0), bank(1)]
-            for c in range(2):
-                xw = x[i][:, c, :].bitcast(F32)
+                xt = tpsum.tile([P, 4 * P], F32, tag="xt")
+                xw = xr[:].bitcast(F32)
                 for j in range(4):
-                    nc.tensor.transpose(
-                        out=xt[i][c][:, j * P : (j + 1) * P], in_=xw[:, j * P : (j + 1) * P], identity=ident[:]
-                    )
-
-        def add_squares(i):
-            nc.gpsimd.tensor_tensor(out=sa[i][:], in0=sa[i][:], in1=sb[i][:], op=ALU.add)
-            nc.gpsimd.tensor_tensor(out=sr[i][:], in0=sr[i][:], in1=si[i][:], op=ALU.add)
-
-        def evacuate(i):
-            gt[i] = work.tile([P, 2, HALF], F32, name="g", tag="g", bufs=2, align_bytes=64)
-            nc.vector.tensor_copy(
-                out=gt[i][:, 0, :].rearrange("p (g r u) -> p g r u", g=2, u=2),
-                in_=xt[i][0][:].rearrange("p (g u r) -> p g r u", g=2, u=2),
-            )
-            nc.vector.tensor_copy(out=gt[i][:, 1, :], in_=xt[i][1][:])
-
-        def quantise(i):
-            nc.vector.quantize_mx(
-                out=xcodes[:, i, :].bitcast(FP8X4), scales=xscales[:, i, :], in_=gt[i][:, 0, :].bitcast(BF16)
-            )
-
-        def transpose_back(i):
-            b = 2 + 2 * (i % 2)
-            xps[i] = [bank(b), bank(b + 1)]
-            gw = gt[i][:, 0, :].rearrange("p (g r u) -> p g r u", g=2, u=2)
-            for g in range(2):
-                for u in range(2):
-                    j = 2 * g + u
-                    nc.tensor.transpose(out=xps[i][0][:, j * P : (j + 1) * P], in_=gw[:, g, :, u], identity=ident[:])
-            for j in range(4):
-                nc.tensor.transpose(
-                    out=xps[i][1][:, j * P : (j + 1) * P], in_=gt[i][:, 1, j * P : (j + 1) * P], identity=ident[:]
+                    nc.tensor.transpose(out=xt[:, j * P : (j + 1) * P], in_=xw[:, j * P : (j + 1) * P], identity=ident[:])
+                grouped = worka.tile([P, 2, P, 4], BF16, tag="grouped", align_bytes=64)
+                nc.scalar.copy(
+                    out=grouped[:].bitcast(F32),
+                    in_=xt[:].rearrange("p (g u r) -> p g r u", g=2, u=2),
                 )
 
-        def rsqrts(i):
-            nc.scalar.activation(out=sa[i][:], in_=sa[i][:], func=ACT.Abs_reciprocal_sqrt)
-            nc.scalar.activation(
-                out=sr[i][:], in_=sr[i][:], func=ACT.Abs_reciprocal_sqrt, bias=eps_t[:, 0:1], scale=1.0
-            )
-
-        def phase_sums(i):
-            junk = big("j", 1, F32)
-            nc.vector.scalar_tensor_tensor(
-                out=junk[:], in0=xps[i][0][:].bitcast(BF16), scalar=EPS, in1=sa[i][:], op0=ALU.add, op1=ALU.mult,
-                accum_out=sc[:, i : i + 1],
-            )
-            nc.vector.scalar_tensor_tensor(
-                out=junk[:], in0=xps[i][1][:].bitcast(BF16), scalar=EPS, in1=sa[i][:], op0=ALU.add, op1=ALU.mult,
-                accum_out=ss[:, i : i + 1],
-            )
-
-        def normalise(i):
-            nc.vector.tensor_tensor(out=cr_all[i][:], in0=xps[i][0][:].bitcast(BF16), in1=sr[i][:], op=ALU.mult)
-            nc.vector.scalar_tensor_tensor(
-                out=nci_all[i][:], in0=xps[i][1][:].bitcast(BF16), scalar=-1.0, in1=sr[i][:], op0=ALU.mult, op1=ALU.mult
-            )
-
-        def gains(lo, hi):
-            cols = slice(lo, hi)
-            nc.vector.tensor_tensor(out=sc[:, cols], in0=sc[:, cols], in1=sc[:, cols], op=ALU.mult)
-            nc.vector.tensor_tensor(out=ss[:, cols], in0=ss[:, cols], in1=ss[:, cols], op=ALU.mult)
-            nc.vector.tensor_tensor(out=sc[:, cols], in0=sc[:, cols], in1=ss[:, cols], op=ALU.add)
-            nc.vector.tensor_scalar(
-                out=sc[:, cols], in0=sc[:, cols], scalar1=-1.0 / (D * D), scalar2=1.0, op0=ALU.mult, op1=ALU.add
-            )
-            nc.vector.tensor_scalar(
-                out=gp[:, cols], in0=sc[:, cols], scalar1=cf32[:, 0:1], scalar2=1.0 / (2.0 * math.pi), op0=ALU.mult,
-                op1=ALU.mult,
-            )
-
-        def product(i):
-            b = 2 * (i % 3)
-            p0[i] = [bank(b), bank(b + 1)]
-            for n in range(2):
-                for g in range(2):
-                    nc.tensor.matmul_mx(
-                        out=p0[i][n][:],
-                        lhsT=xcodes[:, i, g * P : (g + 1) * P].bitcast(FP8X4),
-                        lhsT_scale=xscales[:, i, g * P : (g + 1) * P],
-                        rhs=pcodes[:, g, n * HALF : (n + 1) * HALF].bitcast(FP8X4),
-                        rhs_scale=pscales[:, g, n * HALF : (n + 1) * HALF],
-                        start=(g == 0),
-                        stop=(g == 1),
-                    )
-
-        def reduce_range(i):
-            g_i = gp[:, i : i + 1]
-            ki = big("j", 1, I32)
-            vs[i] = big("x", 3, F32)
-            for n in range(2):
-                cols = slice(n * HALF, (n + 1) * HALF)
-                nc.vector.tensor_scalar(out=ki[:, cols], in0=p0[i][n][:], scalar1=g_i, scalar2=None, op0=ALU.mult)
-            for n in range(2):
-                cols = slice(n * HALF, (n + 1) * HALF)
+                sa = worka.tile([P, D], F32, tag="sa")
+                sb = worka.tile([P, D], F32, tag="sb")
+                sr = worka.tile([P, D], F32, tag="sr")
+                si = worka.tile([P, D], F32, tag="si")
+                nc.scalar.activation(out=sa[:], in_=xr[:], func=ACT.Square, bias=eps_t[:, 0:1], scale=1.0)
+                nc.scalar.activation(out=sb[:], in_=xi[:], func=ACT.Square, bias=eps_t[:, 0:1], scale=1.0)
+                nc.scalar.activation(out=sr[:], in_=xr[:], func=ACT.Square)
+                nc.scalar.activation(out=si[:], in_=xi[:], func=ACT.Square)
+                nc.vector.tensor_tensor(out=sa[:], in0=sa[:], in1=sb[:], op=ALU.add)
+                nc.vector.tensor_tensor(out=sr[:], in0=sr[:], in1=si[:], op=ALU.add)
+                nc.vector.quantize_mx(
+                    out=xcodes[:, i, :].bitcast(FP8X4),
+                    scales=xscales[:, i, :],
+                    in_=grouped[:].rearrange("p g r t -> p (g r t)"),
+                )
+                nc.scalar.activation(out=sa[:], in_=sa[:], func=ACT.Abs_reciprocal_sqrt)
+                nc.scalar.activation(out=sr[:], in_=sr[:], func=ACT.Abs_reciprocal_sqrt, bias=eps_t[:, 0:1], scale=1.0)
                 nc.vector.scalar_tensor_tensor(
-                    out=vs[i][:, cols], in0=p0[i][n][:], scalar=g_i, in1=ki[:, cols], op0=ALU.mult, op1=ALU.subtract
+                    out=sb[:], in0=xr[:], scalar=EPS, in1=sa[:], op0=ALU.add, op1=ALU.mult, accum_out=sc[:, i : i + 1]
+                )
+                nc.vector.scalar_tensor_tensor(
+                    out=si[:], in0=xi[:], scalar=EPS, in1=sa[:], op0=ALU.add, op1=ALU.mult, accum_out=ss[:, i : i + 1]
+                )
+                nc.vector.tensor_tensor(out=cr_all[i][:], in0=xr[:], in1=sr[:], op=ALU.mult)
+                nc.vector.scalar_tensor_tensor(
+                    out=nci_all[i][:], in0=xi[:], scalar=-1.0, in1=sr[:], op0=ALU.mult, op1=ALU.mult
                 )
 
-        def sines(i):
-            hh[i] = big("g", 2, F32)
-            nc.scalar.activation(out=hh[i][:], in_=vs[i][:], func=ACT.Sin, scale=math.pi)
-            nc.scalar.activation(out=vs[i][:], in_=vs[i][:], func=ACT.Sin, scale=2.0 * math.pi)
-            nc.scalar.activation(out=hh[i][:], in_=hh[i][:], func=ACT.Square, scale=math.sqrt(2.0))
-
-        def sine_product_a(i):
-            sa2[i] = big("sa", 3, F32)
-            nc.gpsimd.tensor_tensor(out=sa2[i][:], in0=vs[i][:], in1=cr_all[i][:], op=ALU.mult)
-
-        def sine_product_b(i):
-            sb2[i] = big("sr", 3, F32)
-            nc.gpsimd.tensor_tensor(out=sb2[i][:], in0=vs[i][:], in1=nci_all[i][:], op=ALU.mult)
-
-        def rotate(i):
-            fa[i] = big("sb", 2, F32)
-            fb[i] = big("si", 2, F32)
-            nc.vector.scalar_tensor_tensor(
-                out=fa[i][:], in0=hh[i][:], scalar=1.0, in1=cr_all[i][:], op0=ALU.subtract, op1=ALU.mult
+            nc.vector.tensor_tensor(out=sc[:], in0=sc[:], in1=sc[:], op=ALU.mult)
+            nc.vector.tensor_tensor(out=ss[:], in0=ss[:], in1=ss[:], op=ALU.mult)
+            nc.vector.tensor_tensor(out=sc[:], in0=sc[:], in1=ss[:], op=ALU.add)
+            nc.vector.tensor_scalar(
+                out=sc[:], in0=sc[:], scalar1=-1.0 / (D * D), scalar2=1.0, op0=ALU.mult, op1=ALU.add
             )
-            nc.vector.scalar_tensor_tensor(
-                out=fb[i][:], in0=hh[i][:], scalar=1.0, in1=nci_all[i][:], op0=ALU.subtract, op1=ALU.mult
-            )
-            sums[i] = stat.tile([P, 2], F32, name="sums", tag="sums")
-            nc.vector.scalar_tensor_tensor(
-                out=sb2[i][:], in0=sb2[i][:], scalar=1.0, in1=fa[i][:], op0=ALU.mult, op1=ALU.subtract,
-                accum_out=sums[i][:, 0:1],
-            )
-            nc.vector.scalar_tensor_tensor(
-                out=sa2[i][:], in0=sa2[i][:], scalar=1.0, in1=fb[i][:], op0=ALU.mult, op1=ALU.add,
-                accum_out=sums[i][:, 1:2],
+            nc.vector.tensor_scalar(
+                out=gp[:], in0=sc[:], scalar1=cf32[:, 0:1], scalar2=1.0 / (2.0 * math.pi), op0=ALU.mult, op1=ALU.mult
             )
 
-        def minus_means(i):
-            nmu[i] = stat.tile([P, 2], F32, name="nmu", tag="nmu")
-            nc.gpsimd.tensor_scalar(
-                out=nmu[i][:], in0=sums[i][:], scalar1=-1.0 / D, scalar2=0.0, op0=ALU.mult, op1=ALU.add
-            )
+        with tc.tile_pool(name="workb", bufs=2) as workb, tc.tile_pool(name="stat", bufs=4) as stat, tc.psum_pool(
+            name="ppsum", bufs=2
+        ) as ppsum, tc.manual_schedule():
+            p0 = {}
+            vs = {}
+            hh = {}
+            fa = {}
+            fb = {}
+            sa2 = {}
+            sb2 = {}
+            sums = {}
+            nmu = {}
+            sq = {}
+            rstd = {}
+            ot = {}
 
-        def squared_deviations(i):
-            sq[i] = stat.tile([P, 2], F32, name="sq", tag="sq")
-            nc.scalar.activation(
-                out=hh[i][:], in_=sb2[i][:], func=ACT.Square, bias=nmu[i][:, 0:1], scale=1.0, accum_out=sq[i][:, 0:1]
-            )
-            nc.scalar.activation(
-                out=hh[i][:], in_=sa2[i][:], func=ACT.Square, bias=nmu[i][:, 1:2], scale=1.0, accum_out=sq[i][:, 1:2]
-            )
+            def valid(i):
+                return 0 <= i < NT
 
-        def inverse_deviations(i):
-            var = stat.tile([P, 2], F32, name="var", tag="var")
-            rstd[i] = stat.tile([P, 2], F32, name="rstd", tag="rstd")
-            nc.gpsimd.tensor_scalar(out=var[:], in0=sq[i][:], scalar1=1.0 / D, scalar2=EPS, op0=ALU.mult, op1=ALU.add)
-            nc.gpsimd.tensor_tensor(out=rstd[i][:], in0=var[:], in1=neghalf[:], op=ALU.pow)
+            def there(i, half):
+                t1 = ppsum.tile([P, HALF], F32, name="t1", tag="t1", bufs=1)
+                for jj in range(4):
+                    j = 4 * half + jj
+                    nc.tensor.transpose(
+                        out=t1[:, jj * P : (jj + 1) * P], in_=sa2[i][:, j * P : (j + 1) * P], identity=ident[:]
+                    )
+                for jj in range(4):
+                    j = 4 * half + jj
+                    nc.scalar.activation(
+                        out=ot[i][:, j, :], in_=t1[:, jj * P : (jj + 1) * P], func=ACT.Identity,
+                        bias=wbt[:, 8 + j : 9 + j], scale=wbt[:, j : j + 1],
+                    )
 
-        def scale_shift_store(i):
-            nc.vector.scalar_tensor_tensor(
-                out=fa[i][:], in0=sb2[i][:], scalar=nmu[i][:, 0:1], in1=wps[:], op0=ALU.add, op1=ALU.mult
-            )
-            nc.vector.scalar_tensor_tensor(
-                out=fa[i][:], in0=fa[i][:], scalar=rstd[i][:, 0:1], in1=bps[:], op0=ALU.mult, op1=ALU.add
-            )
-            nc.sync.dma_start(out=o0_d[i], in_=fa[i][:])
-            nc.vector.scalar_tensor_tensor(
-                out=fb[i][:], in0=sa2[i][:], scalar=nmu[i][:, 1:2], in1=wps[:], op0=ALU.add, op1=ALU.mult
-            )
-            nc.vector.scalar_tensor_tensor(
-                out=fb[i][:], in0=fb[i][:], scalar=rstd[i][:, 1:2], in1=bps[:], op0=ALU.mult, op1=ALU.add
-            )
-            nc.sync.dma_start(out=o1_d[i], in_=fb[i][:])
+            def back(i, half):
+                t2 = ppsum.tile([P, HALF], F32, name="t2", tag="t2", bufs=1)
+                for jj in range(4):
+                    j = 4 * half + jj
+                    nc.tensor.transpose(out=t2[:, jj * P : (jj + 1) * P], in_=ot[i][:, j, :], identity=ident[:])
+                nc.scalar.copy(out=fb[i][:, half * HALF : (half + 1) * HALF], in_=t2[:])
 
-        def ok(i):
-            return 0 <= i < NT
-
-        with tc.manual_schedule():
-            for k in range(-2, NT + 1):
-                if ok(k + 2):
-                    load(k + 2)
-                if k == 0:
-                    p_load()
-                if ok(k + 1):
-                    squares(k + 1)
-                    transpose_there(k + 1)
-                    add_squares(k + 1)
-                if k == NT - 1:
-                    product(0)
-                    reduce_range(0)
-                if k == NT:
-                    product(1)
-                    reduce_range(1)
-                if ok(k - 1):
-                    phase_sums(k - 1)
-                if ok(k):
-                    quantise(k)
-                if ok(k - 1):
-                    normalise(k - 1)
-                if ok(k + 1):
-                    evacuate(k + 1)
-                if 1 <= k <= 4:
-                    p_quantise(k - 1)
-                if k == NT // 2:
-                    gains(0, NT // 2)
-                if ok(k):
-                    transpose_back(k)
-                    rsqrts(k)
-            gains(NT // 2, NT)
-            sines(0)
-            sine_product_a(0)
-            sine_product_b(0)
-            sines(1)
-            sine_product_a(1)
-            product(2)
-            reduce_range(2)
-            for k in range(0, NT + 1):
-                if ok(k + 3):
-                    product(k + 3)
-                if ok(k):
-                    rotate(k)
-                    minus_means(k)
-                if k >= 1 and ok(k + 1):
-                    sines(k + 1)
-                if ok(k):
-                    squared_deviations(k)
-                if ok(k - 1):
-                    scale_shift_store(k - 1)
-                if k >= 1 and ok(k + 1):
-                    sine_product_a(k + 1)
-                if k == 0:
-                    sine_product_b(1)
-                if ok(k):
-                    inverse_deviations(k)
-                if k >= 1 and ok(k + 1):
-                    sine_product_b(k + 1)
-                if ok(k + 3):
-                    reduce_range(k + 3)
+            for k in range(-3, NT + 1):
+                i = k + 3
+                if valid(i):
+                    p0[i] = [ppsum.tile([P, HALF], F32, name="p0_%d" % n, tag="p0_%d" % n) for n in range(2)]
+                    for n in range(2):
+                        for g in range(2):
+                            nc.tensor.matmul_mx(
+                                out=p0[i][n][:],
+                                lhsT=xcodes[:, i, g * P : (g + 1) * P].bitcast(FP8X4),
+                                lhsT_scale=xscales[:, i, g * P : (g + 1) * P],
+                                rhs=pcodes[:, g, n * HALF : (n + 1) * HALF].bitcast(FP8X4),
+                                rhs_scale=pscales[:, g, n * HALF : (n + 1) * HALF],
+                                start=(g == 0),
+                                stop=(g == 1),
+                            )
+                i = k - 1
+                if valid(i):
+                    nc.vector.tensor_scalar(
+                        out=sa2[i][:], in0=sa2[i][:], scalar1=nmu[i][:, 1:2], scalar2=rstd[i][:, 1:2], op0=ALU.add,
+                        op1=ALU.mult,
+                    )
+                i = k
+                if valid(i):
+                    fa[i] = workb.tile([P, D], F32, name="fa", tag="fa")
+                    fb[i] = workb.tile([P, D], F32, name="fb", tag="fb")
+                    nc.vector.scalar_tensor_tensor(
+                        out=fa[i][:], in0=hh[i][:], scalar=1.0, in1=cr_all[i][:], op0=ALU.subtract, op1=ALU.mult
+                    )
+                    nc.vector.scalar_tensor_tensor(
+                        out=fb[i][:], in0=hh[i][:], scalar=1.0, in1=nci_all[i][:], op0=ALU.subtract, op1=ALU.mult
+                    )
+                    sums[i] = stat.tile([P, 2], F32, name="sums", tag="sums")
+                    nc.vector.scalar_tensor_tensor(
+                        out=sb2[i][:], in0=sb2[i][:], scalar=1.0, in1=fa[i][:], op0=ALU.mult, op1=ALU.subtract,
+                        accum_out=sums[i][:, 0:1],
+                    )
+                    nc.vector.scalar_tensor_tensor(
+                        out=sa2[i][:], in0=sa2[i][:], scalar=1.0, in1=fb[i][:], op0=ALU.mult, op1=ALU.add,
+                        accum_out=sums[i][:, 1:2],
+                    )
+                    nmu[i] = stat.tile([P, 2], F32, name="nmu", tag="nmu")
+                    nc.gpsimd.tensor_scalar(
+                        out=nmu[i][:], in0=sums[i][:], scalar1=-1.0 / D, scalar2=0.0, op0=ALU.mult, op1=ALU.add
+                    )
+                if valid(k + 1):
+                    i = k + 1
+                    hh[i] = workb.tile([P, D], F32, name="hh", tag="hh")
+                    nc.scalar.activation(out=hh[i][:], in_=vs[i][:], func=ACT.Sin, scale=math.pi)
+                    nc.scalar.activation(out=vs[i][:], in_=vs[i][:], func=ACT.Sin, scale=2.0 * math.pi)
+                if valid(k - 1):
+                    ot[k - 1] = workb.tile([P, 8, P], F32, name="ot", tag="ot", bufs=1)
+                    there(k - 1, 0)
+                if valid(k + 1):
+                    i = k + 1
+                    nc.scalar.activation(out=hh[i][:], in_=hh[i][:], func=ACT.Square, scale=math.sqrt(2.0))
+                if valid(k - 1):
+                    back(k - 1, 0)
+                    there(k - 1, 1)
+                i = k
+                if valid(i):
+                    sq[i] = stat.tile([P, 2], F32, name="sq", tag="sq")
+                    nc.scalar.activation(
+                        out=hh[i][:], in_=sb2[i][:], func=ACT.Square, bias=nmu[i][:, 0:1], scale=1.0,
+                        accum_out=sq[i][:, 0:1],
+                    )
+                    nc.scalar.activation(
+                        out=hh[i][:], in_=sa2[i][:], func=ACT.Square, bias=nmu[i][:, 1:2], scale=1.0,
+                        accum_out=sq[i][:, 1:2],
+                    )
+                if valid(k - 1):
+                    back(k - 1, 1)
+                    nc.sync.dma_start(out=o1_d[k - 1], in_=fb[k - 1][:])
+                i = k - 1
+                if valid(i):
+                    nc.vector.scalar_tensor_tensor(
+                        out=fa[i][:], in0=sb2[i][:], scalar=nmu[i][:, 0:1], in1=wps[:], op0=ALU.add, op1=ALU.mult
+                    )
+                    nc.vector.scalar_tensor_tensor(
+                        out=fa[i][:], in0=fa[i][:], scalar=rstd[i][:, 0:1], in1=bps[:], op0=ALU.mult, op1=ALU.add
+                    )
+                    nc.sync.dma_start(out=o0_d[i], in_=fa[i][:])
+                i = k + 1
+                if valid(i):
+                    sa2[i] = workb.tile([P, D], F32, name="sa2", tag="sa2", bufs=3)
+                    nc.gpsimd.tensor_tensor(out=sa2[i][:], in0=vs[i][:], in1=cr_all[i][:], op=ALU.mult)
+                i = k
+                if valid(i):
+                    var = stat.tile([P, 2], F32, name="var", tag="var")
+                    rstd[i] = stat.tile([P, 2], F32, name="rstd", tag="rstd")
+                    nc.gpsimd.tensor_scalar(
+                        out=var[:], in0=sq[i][:], scalar1=1.0 / D, scalar2=EPS, op0=ALU.mult, op1=ALU.add
+                    )
+                    nc.gpsimd.tensor_tensor(out=rstd[i][:], in0=var[:], in1=neghalf[:], op=ALU.pow)
+                i = k + 1
+                if valid(i):
+                    sb2[i] = workb.tile([P, D], F32, name="sb2", tag="sb2", bufs=3)
+                    nc.gpsimd.tensor_tensor(out=sb2[i][:], in0=vs[i][:], in1=nci_all[i][:], op=ALU.mult)
+                i = k + 2
+                if valid(i):
+                    g_i = gp[:, i : i + 1]
+                    ki = workb.tile([P, D], I32, name="ki", tag="ki", bufs=1)
+                    vs[i] = workb.tile([P, D], F32, name="vs", tag="vs")
+                    for n in range(2):
+                        cols = slice(n * HALF, (n + 1) * HALF)
+                        nc.vector.tensor_scalar(
+                            out=ki[:, cols], in0=p0[i][n][:], scalar1=g_i, scalar2=None, op0=ALU.mult
+                        )
+                    for n in range(2):
+                        cols = slice(n * HALF, (n + 1) * HALF)
+                        nc.vector.scalar_tensor_tensor(
+                            out=vs[i][:, cols], in0=p0[i][n][:], scalar=g_i, in1=ki[:, cols], op0=ALU.mult,
+                            op1=ALU.subtract,
+                        )

@@ -191,6 +191,9 @@ def tile_quantumcoherencelayer_kernel(
             def valid(i):
                 return 0 <= i < NT
 
+            def turned(i):
+                return 0 <= i < NT - 1
+
             def there(i, half):
                 t1 = ppsum.tile([P, HALF], F32, name="t1", tag="t1", bufs=1)
                 for jj in range(4):
@@ -227,22 +230,24 @@ def tile_quantumcoherencelayer_kernel(
                                 start=(g == 0),
                                 stop=(g == 1),
                             )
-                i = k - 1
-                if valid(i):
-                    nc.vector.tensor_scalar(
-                        out=sa2[i][:], in0=sa2[i][:], scalar1=nmu[i][:, 1:2], scalar2=rstd[i][:, 1:2], op0=ALU.add,
-                        op1=ALU.mult,
-                    )
                 i = k
                 if valid(i):
-                    fa[i] = workb.tile([P, D], F32, name="fa", tag="fa")
-                    fb[i] = workb.tile([P, D], F32, name="fb", tag="fb")
+                    fa[i] = workb.tile([P, D], F32, name="fa", tag="fa", bufs=3)
+                    fb[i] = workb.tile([P, D], F32, name="fb", tag="fb", bufs=3)
                     nc.vector.scalar_tensor_tensor(
                         out=fa[i][:], in0=hh[i][:], scalar=1.0, in1=cr_all[i][:], op0=ALU.subtract, op1=ALU.mult
                     )
                     nc.vector.scalar_tensor_tensor(
                         out=fb[i][:], in0=hh[i][:], scalar=1.0, in1=nci_all[i][:], op0=ALU.subtract, op1=ALU.mult
                     )
+                i = k - 1
+                if turned(i):
+                    nc.vector.tensor_scalar(
+                        out=sa2[i][:], in0=sa2[i][:], scalar1=nmu[i][:, 1:2], scalar2=rstd[i][:, 1:2], op0=ALU.add,
+                        op1=ALU.mult,
+                    )
+                i = k
+                if valid(i):
                     sums[i] = stat.tile([P, 2], F32, name="sums", tag="sums")
                     nc.vector.scalar_tensor_tensor(
                         out=sb2[i][:], in0=sb2[i][:], scalar=1.0, in1=fa[i][:], op0=ALU.mult, op1=ALU.subtract,
@@ -261,15 +266,15 @@ def tile_quantumcoherencelayer_kernel(
                     hh[i] = workb.tile([P, D], F32, name="hh", tag="hh")
                     nc.scalar.activation(out=hh[i][:], in_=vs[i][:], func=ACT.Sin, scale=math.pi)
                     nc.scalar.activation(out=vs[i][:], in_=vs[i][:], func=ACT.Sin, scale=2.0 * math.pi)
-                if valid(k - 1):
+                if turned(k - 2):
+                    back(k - 2, 1)
+                    nc.sync.dma_start(out=o1_d[k - 2], in_=fb[k - 2][:])
+                if turned(k - 1):
                     ot[k - 1] = workb.tile([P, 8, P], F32, name="ot", tag="ot", bufs=1)
                     there(k - 1, 0)
                 if valid(k + 1):
                     i = k + 1
                     nc.scalar.activation(out=hh[i][:], in_=hh[i][:], func=ACT.Square, scale=math.sqrt(2.0))
-                if valid(k - 1):
-                    back(k - 1, 0)
-                    there(k - 1, 1)
                 i = k
                 if valid(i):
                     sq[i] = stat.tile([P, 2], F32, name="sq", tag="sq")
@@ -281,9 +286,9 @@ def tile_quantumcoherencelayer_kernel(
                         out=hh[i][:], in_=sa2[i][:], func=ACT.Square, bias=nmu[i][:, 1:2], scale=1.0,
                         accum_out=sq[i][:, 1:2],
                     )
-                if valid(k - 1):
-                    back(k - 1, 1)
-                    nc.sync.dma_start(out=o1_d[k - 1], in_=fb[k - 1][:])
+                if turned(k - 1):
+                    back(k - 1, 0)
+                    there(k - 1, 1)
                 i = k - 1
                 if valid(i):
                     nc.vector.scalar_tensor_tensor(
@@ -293,6 +298,14 @@ def tile_quantumcoherencelayer_kernel(
                         out=fa[i][:], in0=fa[i][:], scalar=rstd[i][:, 0:1], in1=bps[:], op0=ALU.mult, op1=ALU.add
                     )
                     nc.sync.dma_start(out=o0_d[i], in_=fa[i][:])
+                if i == NT - 1:
+                    nc.vector.scalar_tensor_tensor(
+                        out=fb[i][:], in0=sa2[i][:], scalar=nmu[i][:, 1:2], in1=wps[:], op0=ALU.add, op1=ALU.mult
+                    )
+                    nc.vector.scalar_tensor_tensor(
+                        out=fb[i][:], in0=fb[i][:], scalar=rstd[i][:, 1:2], in1=bps[:], op0=ALU.mult, op1=ALU.add
+                    )
+                    nc.sync.dma_start(out=o1_d[i], in_=fb[i][:])
                 i = k + 1
                 if valid(i):
                     sa2[i] = workb.tile([P, D], F32, name="sa2", tag="sa2", bufs=3)

@@ -19,6 +19,7 @@ ROWS = 2048
 NT = ROWS // P
 HALF = 512
 EPS = 1e-8
+POOL_COLS = 384
 FLOPS = 2 * ROWS * D * D
 
 
@@ -230,6 +231,11 @@ def tile_quantumcoherencelayer_kernel(
                                 start=(g == 0),
                                 stop=(g == 1),
                             )
+                if valid(k + 1):
+                    i = k + 1
+                    hh[i] = workb.tile([P, D], F32, name="hh", tag="hh")
+                    nc.scalar.activation(out=hh[i][:], in_=vs[i][:], func=ACT.Sin, scale=math.pi)
+                    nc.scalar.activation(out=vs[i][:], in_=vs[i][:], func=ACT.Sin, scale=2.0 * math.pi)
                 i = k
                 if valid(i):
                     fa[i] = workb.tile([P, D], F32, name="fa", tag="fa", bufs=3)
@@ -253,6 +259,13 @@ def tile_quantumcoherencelayer_kernel(
                         out=sb2[i][:], in0=sb2[i][:], scalar=1.0, in1=fa[i][:], op0=ALU.mult, op1=ALU.subtract,
                         accum_out=sums[i][:, 0:1],
                     )
+                if valid(k + 1):
+                    sb2[k + 1] = workb.tile([P, D], F32, name="sb2", tag="sb2", bufs=3)
+                    nc.vector.tensor_tensor(
+                        out=sb2[k + 1][:, POOL_COLS:D], in0=vs[k + 1][:, POOL_COLS:D], in1=nci_all[k + 1][:, POOL_COLS:D],
+                        op=ALU.mult,
+                    )
+                if valid(i):
                     nc.vector.scalar_tensor_tensor(
                         out=sa2[i][:], in0=sa2[i][:], scalar=1.0, in1=fb[i][:], op0=ALU.mult, op1=ALU.add,
                         accum_out=sums[i][:, 1:2],
@@ -261,11 +274,6 @@ def tile_quantumcoherencelayer_kernel(
                     nc.gpsimd.tensor_scalar(
                         out=nmu[i][:], in0=sums[i][:], scalar1=-1.0 / D, scalar2=0.0, op0=ALU.mult, op1=ALU.add
                     )
-                if valid(k + 1):
-                    i = k + 1
-                    hh[i] = workb.tile([P, D], F32, name="hh", tag="hh")
-                    nc.scalar.activation(out=hh[i][:], in_=vs[i][:], func=ACT.Sin, scale=math.pi)
-                    nc.scalar.activation(out=vs[i][:], in_=vs[i][:], func=ACT.Sin, scale=2.0 * math.pi)
                 if turned(k - 2):
                     back(k - 2, 1)
                     nc.sync.dma_start(out=o1_d[k - 2], in_=fb[k - 2][:])
@@ -320,8 +328,9 @@ def tile_quantumcoherencelayer_kernel(
                     nc.gpsimd.tensor_tensor(out=rstd[i][:], in0=var[:], in1=neghalf[:], op=ALU.pow)
                 i = k + 1
                 if valid(i):
-                    sb2[i] = workb.tile([P, D], F32, name="sb2", tag="sb2", bufs=3)
-                    nc.gpsimd.tensor_tensor(out=sb2[i][:], in0=vs[i][:], in1=nci_all[i][:], op=ALU.mult)
+                    nc.gpsimd.tensor_tensor(
+                        out=sb2[i][:, 0:POOL_COLS], in0=vs[i][:, 0:POOL_COLS], in1=nci_all[i][:, 0:POOL_COLS], op=ALU.mult
+                    )
                 i = k + 2
                 if valid(i):
                     g_i = gp[:, i : i + 1]

@@ -19,7 +19,7 @@ ROWS = 2048
 NT = ROWS // P
 HALF = 512
 EPS = 1e-8
-POOL_COLS = 384
+POOL_COLS = 640
 FLOPS = 2 * ROWS * D * D
 
 
@@ -188,6 +188,7 @@ def tile_quantumcoherencelayer_kernel(
             sq = {}
             rstd = {}
             ot = {}
+            var = {}
 
             def valid(i):
                 return 0 <= i < NT
@@ -214,7 +215,7 @@ def tile_quantumcoherencelayer_kernel(
                 for jj in range(4):
                     j = 4 * half + jj
                     nc.tensor.transpose(out=t2[:, jj * P : (jj + 1) * P], in_=ot[i][:, j, :], identity=ident[:])
-                nc.scalar.copy(out=fb[i][:, half * HALF : (half + 1) * HALF], in_=t2[:])
+                nc.scalar.copy(out=sa2[i][:, half * HALF : (half + 1) * HALF], in_=t2[:])
 
             for k in range(-3, NT + 1):
                 i = k + 3
@@ -239,7 +240,7 @@ def tile_quantumcoherencelayer_kernel(
                 i = k
                 if valid(i):
                     fa[i] = workb.tile([P, D], F32, name="fa", tag="fa", bufs=3)
-                    fb[i] = workb.tile([P, D], F32, name="fb", tag="fb", bufs=3)
+                    fb[i] = workb.tile([P, D], F32, name="fb", tag="o%d" % (i % 4), bufs=1)
                     nc.vector.scalar_tensor_tensor(
                         out=fa[i][:], in0=hh[i][:], scalar=1.0, in1=cr_all[i][:], op0=ALU.subtract, op1=ALU.mult
                     )
@@ -271,12 +272,10 @@ def tile_quantumcoherencelayer_kernel(
                         accum_out=sums[i][:, 1:2],
                     )
                     nmu[i] = stat.tile([P, 2], F32, name="nmu", tag="nmu")
-                    nc.gpsimd.tensor_scalar(
-                        out=nmu[i][:], in0=sums[i][:], scalar1=-1.0 / D, scalar2=0.0, op0=ALU.mult, op1=ALU.add
-                    )
+                    nc.vector.tensor_scalar(out=nmu[i][:], in0=sums[i][:], scalar1=-1.0 / D, scalar2=None, op0=ALU.mult)
                 if turned(k - 2):
                     back(k - 2, 1)
-                    nc.sync.dma_start(out=o1_d[k - 2], in_=fb[k - 2][:])
+                    nc.sync.dma_start(out=o1_d[k - 2], in_=sa2[k - 2][:])
                 if turned(k - 1):
                     ot[k - 1] = workb.tile([P, 8, P], F32, name="ot", tag="ot", bufs=1)
                     there(k - 1, 0)
@@ -294,6 +293,8 @@ def tile_quantumcoherencelayer_kernel(
                         out=hh[i][:], in_=sa2[i][:], func=ACT.Square, bias=nmu[i][:, 1:2], scale=1.0,
                         accum_out=sq[i][:, 1:2],
                     )
+                    var[i] = stat.tile([P, 2], F32, name="var", tag="var")
+                    nc.scalar.activation(out=var[i][:], in_=sq[i][:], func=ACT.Identity, bias=eps_t[:, 0:1], scale=1.0 / D)
                 if turned(k - 1):
                     back(k - 1, 0)
                     there(k - 1, 1)
@@ -308,24 +309,20 @@ def tile_quantumcoherencelayer_kernel(
                     nc.sync.dma_start(out=o0_d[i], in_=fa[i][:])
                 if i == NT - 1:
                     nc.vector.scalar_tensor_tensor(
-                        out=fb[i][:], in0=sa2[i][:], scalar=nmu[i][:, 1:2], in1=wps[:], op0=ALU.add, op1=ALU.mult
+                        out=sa2[i][:], in0=sa2[i][:], scalar=nmu[i][:, 1:2], in1=wps[:], op0=ALU.add, op1=ALU.mult
                     )
                     nc.vector.scalar_tensor_tensor(
-                        out=fb[i][:], in0=fb[i][:], scalar=rstd[i][:, 1:2], in1=bps[:], op0=ALU.mult, op1=ALU.add
+                        out=sa2[i][:], in0=sa2[i][:], scalar=rstd[i][:, 1:2], in1=bps[:], op0=ALU.mult, op1=ALU.add
                     )
-                    nc.sync.dma_start(out=o1_d[i], in_=fb[i][:])
+                    nc.sync.dma_start(out=o1_d[i], in_=sa2[i][:])
                 i = k + 1
                 if valid(i):
-                    sa2[i] = workb.tile([P, D], F32, name="sa2", tag="sa2", bufs=3)
+                    sa2[i] = workb.tile([P, D], F32, name="sa2", tag="o%d" % ((i - 1) % 4), bufs=1)
                     nc.gpsimd.tensor_tensor(out=sa2[i][:], in0=vs[i][:], in1=cr_all[i][:], op=ALU.mult)
                 i = k
                 if valid(i):
-                    var = stat.tile([P, 2], F32, name="var", tag="var")
                     rstd[i] = stat.tile([P, 2], F32, name="rstd", tag="rstd")
-                    nc.gpsimd.tensor_scalar(
-                        out=var[:], in0=sq[i][:], scalar1=1.0 / D, scalar2=EPS, op0=ALU.mult, op1=ALU.add
-                    )
-                    nc.gpsimd.tensor_tensor(out=rstd[i][:], in0=var[:], in1=neghalf[:], op=ALU.pow)
+                    nc.gpsimd.tensor_tensor(out=rstd[i][:], in0=var[i][:], in1=neghalf[:], op=ALU.pow)
                 i = k + 1
                 if valid(i):
                     nc.gpsimd.tensor_tensor(

@@ -17,9 +17,11 @@ P = 128
 D = 1024
 ROWS = 2048
 NT = ROWS // P
-HALF = 512
+BANK = 512
+PASSES = D // 512
+BLOCKS = D // P
 EPS = 1e-8
-POOL_COLS = 640
+POOL_COLS = 768
 FLOPS = 2 * ROWS * D * D
 
 
@@ -43,25 +45,25 @@ def tile_quantumcoherencelayer_kernel(
         neghalf = keep.tile([P, 2], F32)
         nc.vector.memset(neghalf[:], -0.5)
 
-        cfb = keep.tile([P, 1], BF16)
+        cf_bf = keep.tile([P, 1], BF16)
         with nc.allow_non_contiguous_dma(reason="one bfloat16 scalar to every partition"):
-            nc.scalar.dma_start(out=cfb[:], in_=coherence_factor.partition_broadcast(P))
-        cf32 = keep.tile([P, 1], F32)
-        nc.vector.tensor_copy(out=cf32[:], in_=cfb[:])
+            nc.scalar.dma_start(out=cf_bf[:], in_=coherence_factor.partition_broadcast(P))
+        cf = keep.tile([P, 1], F32)
+        nc.vector.tensor_copy(out=cf[:], in_=cf_bf[:])
 
-        pcodes = keep.tile([P, 2, D], U32, align_bytes=64)
-        pscales = keep.tile([P, 2, D], U8, align_bytes=64)
-        xcodes = keep.tile([P, NT, 2 * P], U32, align_bytes=64)
-        xscales = keep.tile([P, NT, 2 * P], U8, align_bytes=64)
-        sc = keep.tile([P, NT], F32)
-        ss = keep.tile([P, NT], F32)
-        gp = keep.tile([P, NT], F32)
-        wbt = keep.tile([P, 16], F32)
-        cr_all = [keep.tile([P, D], F32, name="cr%d" % i) for i in range(NT)]
-        nci_all = [keep.tile([P, D], F32, name="nci%d" % i) for i in range(NT)]
+        p_codes = keep.tile([P, PASSES, D], U32, align_bytes=64)
+        p_scales = keep.tile([P, PASSES, D], U8, align_bytes=64)
+        x_codes = keep.tile([P, NT, PASSES * P], U32, align_bytes=64)
+        x_scales = keep.tile([P, NT, PASSES * P], U8, align_bytes=64)
+        sum_cos = keep.tile([P, NT], F32)
+        sum_sin = keep.tile([P, NT], F32)
+        gain = keep.tile([P, NT], F32)
+        wb_cols = keep.tile([P, 2 * BLOCKS], F32)
+        unit_re = [keep.tile([P, D], F32, name="cr%d" % i) for i in range(NT)]
+        unit_im_neg = [keep.tile([P, D], F32, name="nci%d" % i) for i in range(NT)]
 
-        wps = cpsum.tile([P, D], BF16)
-        bps = cpsum.tile([P, D], BF16)
+        w_ps = cpsum.tile([P, D], BF16)
+        b_ps = cpsum.tile([P, D], BF16)
 
         with tc.tile_pool(name="stage", bufs=1) as stage, tc.tile_pool(name="xin", bufs=3) as xin, tc.tile_pool(
             name="worka", bufs=2
@@ -74,30 +76,30 @@ def tile_quantumcoherencelayer_kernel(
             nc.vector.memset(ones[:], 1.0)
             for h in range(2):
                 nc.tensor.matmul(
-                    out=wps[:, h * HALF : (h + 1) * HALF],
+                    out=w_ps[:, h * BANK : (h + 1) * BANK],
                     lhsT=ones[:],
-                    rhs=rows[:, h * HALF : (h + 1) * HALF],
+                    rhs=rows[:, h * BANK : (h + 1) * BANK],
                     start=True,
                     stop=True,
                 )
             for h in range(2):
                 nc.tensor.matmul(
-                    out=bps[:, h * HALF : (h + 1) * HALF],
+                    out=b_ps[:, h * BANK : (h + 1) * BANK],
                     lhsT=ones[:],
-                    rhs=rows[:, D + h * HALF : D + (h + 1) * HALF],
+                    rhs=rows[:, D + h * BANK : D + (h + 1) * BANK],
                     start=True,
                     stop=True,
                 )
 
             wb = stage.tile([P, P], BF16)
             nc.vector.memset(wb[:], 0.0)
-            nc.scalar.dma_start(out=wb[0:8, :], in_=ln_weight.rearrange("(j p) -> j p", p=P))
-            nc.scalar.dma_start(out=wb[8:16, :], in_=ln_bias.rearrange("(j p) -> j p", p=P))
+            nc.scalar.dma_start(out=wb[0:BLOCKS, :], in_=ln_weight.rearrange("(j p) -> j p", p=P))
+            nc.scalar.dma_start(out=wb[BLOCKS : 2 * BLOCKS, :], in_=ln_bias.rearrange("(j p) -> j p", p=P))
             wb32 = stage.tile([P, P], F32)
             nc.vector.tensor_copy(out=wb32[:], in_=wb[:])
-            wbt_ps = tpsum.tile([P, 4 * P], F32, tag="xt")
+            wbt_ps = tpsum.tile([P, BANK], F32, tag="xt")
             nc.tensor.transpose(out=wbt_ps[:, 0:P], in_=wb32[:], identity=ident[:])
-            nc.vector.tensor_copy(out=wbt[:], in_=wbt_ps[:, 0:16])
+            nc.vector.tensor_copy(out=wb_cols[:], in_=wbt_ps[:, 0 : 2 * BLOCKS])
 
             for i in range(NT):
                 xr = xin.tile([P, D], BF16, tag="xr")
@@ -106,7 +108,7 @@ def tile_quantumcoherencelayer_kernel(
                 nc.sync.dma_start(out=xi[:], in_=xi_d[i])
 
                 if i == 1:
-                    for g in range(2):
+                    for g in range(PASSES):
                         raw = stage.tile([P, 4, D], BF16, tag="raw")
                         for u in range(2):
                             k0 = 512 * g + 256 * u
@@ -120,75 +122,80 @@ def tile_quantumcoherencelayer_kernel(
                             in_=raw[:].rearrange("p t (c i) -> p c t i", i=4),
                         )
                         nc.vector.quantize_mx(
-                            out=pcodes[:, g, :].bitcast(FP8X4),
-                            scales=pscales[:, g, :],
+                            out=p_codes[:, g, :].bitcast(FP8X4),
+                            scales=p_scales[:, g, :],
                             in_=pg[:].rearrange("p c t -> p (c t)"),
                         )
 
-                xt = tpsum.tile([P, 4 * P], F32, tag="xt")
+                xt = tpsum.tile([P, BANK], F32, tag="xt")
                 xw = xr[:].bitcast(F32)
                 for j in range(4):
                     nc.tensor.transpose(out=xt[:, j * P : (j + 1) * P], in_=xw[:, j * P : (j + 1) * P], identity=ident[:])
-                grouped = worka.tile([P, 2, P, 4], BF16, tag="grouped", align_bytes=64)
+                grouped = worka.tile([P, PASSES, P, 4], BF16, tag="grouped", align_bytes=64)
                 nc.scalar.copy(
                     out=grouped[:].bitcast(F32),
-                    in_=xt[:].rearrange("p (g u r) -> p g r u", g=2, u=2),
+                    in_=xt[:].rearrange("p (g u r) -> p g r u", g=PASSES, u=2),
                 )
 
-                sa = worka.tile([P, D], F32, tag="sa")
-                sb = worka.tile([P, D], F32, tag="sb")
-                sr = worka.tile([P, D], F32, tag="sr")
-                si = worka.tile([P, D], F32, tag="si")
-                nc.scalar.activation(out=sa[:], in_=xr[:], func=ACT.Square, bias=eps_t[:, 0:1], scale=1.0)
-                nc.scalar.activation(out=sb[:], in_=xi[:], func=ACT.Square, bias=eps_t[:, 0:1], scale=1.0)
-                nc.scalar.activation(out=sr[:], in_=xr[:], func=ACT.Square)
-                nc.scalar.activation(out=si[:], in_=xi[:], func=ACT.Square)
-                nc.vector.tensor_tensor(out=sa[:], in0=sa[:], in1=sb[:], op=ALU.add)
-                nc.vector.tensor_tensor(out=sr[:], in0=sr[:], in1=si[:], op=ALU.add)
+                inv_r = worka.tile([P, D], F32, tag="sa")
+                scr_a = worka.tile([P, D], F32, tag="sb")
+                inv_n = worka.tile([P, D], F32, tag="sr")
+                scr_b = worka.tile([P, D], F32, tag="si")
+                nc.scalar.activation(out=inv_r[:], in_=xr[:], func=ACT.Square, bias=eps_t[:, 0:1], scale=1.0)
+                nc.scalar.activation(out=scr_a[:], in_=xi[:], func=ACT.Square, bias=eps_t[:, 0:1], scale=1.0)
+                nc.scalar.activation(out=inv_n[:], in_=xr[:], func=ACT.Square)
+                nc.scalar.activation(out=scr_b[:], in_=xi[:], func=ACT.Square)
+                nc.vector.tensor_tensor(out=inv_r[:], in0=inv_r[:], in1=scr_a[:], op=ALU.add)
+                nc.vector.tensor_tensor(out=inv_n[:], in0=inv_n[:], in1=scr_b[:], op=ALU.add)
                 nc.vector.quantize_mx(
-                    out=xcodes[:, i, :].bitcast(FP8X4),
-                    scales=xscales[:, i, :],
+                    out=x_codes[:, i, :].bitcast(FP8X4),
+                    scales=x_scales[:, i, :],
                     in_=grouped[:].rearrange("p g r t -> p (g r t)"),
                 )
-                nc.scalar.activation(out=sa[:], in_=sa[:], func=ACT.Abs_reciprocal_sqrt)
-                nc.scalar.activation(out=sr[:], in_=sr[:], func=ACT.Abs_reciprocal_sqrt, bias=eps_t[:, 0:1], scale=1.0)
-                nc.vector.scalar_tensor_tensor(
-                    out=sb[:], in0=xr[:], scalar=EPS, in1=sa[:], op0=ALU.add, op1=ALU.mult, accum_out=sc[:, i : i + 1]
+                nc.scalar.activation(out=inv_r[:], in_=inv_r[:], func=ACT.Abs_reciprocal_sqrt)
+                nc.scalar.activation(
+                    out=inv_n[:], in_=inv_n[:], func=ACT.Abs_reciprocal_sqrt, bias=eps_t[:, 0:1], scale=1.0
                 )
                 nc.vector.scalar_tensor_tensor(
-                    out=si[:], in0=xi[:], scalar=EPS, in1=sa[:], op0=ALU.add, op1=ALU.mult, accum_out=ss[:, i : i + 1]
+                    out=scr_a[:], in0=xr[:], scalar=EPS, in1=inv_r[:], op0=ALU.add, op1=ALU.mult,
+                    accum_out=sum_cos[:, i : i + 1],
                 )
-                nc.vector.tensor_tensor(out=cr_all[i][:], in0=xr[:], in1=sr[:], op=ALU.mult)
                 nc.vector.scalar_tensor_tensor(
-                    out=nci_all[i][:], in0=xi[:], scalar=-1.0, in1=sr[:], op0=ALU.mult, op1=ALU.mult
+                    out=scr_b[:], in0=xi[:], scalar=EPS, in1=inv_r[:], op0=ALU.add, op1=ALU.mult,
+                    accum_out=sum_sin[:, i : i + 1],
+                )
+                nc.vector.tensor_tensor(out=unit_re[i][:], in0=xr[:], in1=inv_n[:], op=ALU.mult)
+                nc.vector.scalar_tensor_tensor(
+                    out=unit_im_neg[i][:], in0=xi[:], scalar=-1.0, in1=inv_n[:], op0=ALU.mult, op1=ALU.mult
                 )
 
-            nc.vector.tensor_tensor(out=sc[:], in0=sc[:], in1=sc[:], op=ALU.mult)
-            nc.vector.tensor_tensor(out=ss[:], in0=ss[:], in1=ss[:], op=ALU.mult)
-            nc.vector.tensor_tensor(out=sc[:], in0=sc[:], in1=ss[:], op=ALU.add)
+            nc.vector.tensor_tensor(out=sum_cos[:], in0=sum_cos[:], in1=sum_cos[:], op=ALU.mult)
+            nc.vector.tensor_tensor(out=sum_sin[:], in0=sum_sin[:], in1=sum_sin[:], op=ALU.mult)
+            nc.vector.tensor_tensor(out=sum_cos[:], in0=sum_cos[:], in1=sum_sin[:], op=ALU.add)
             nc.vector.tensor_scalar(
-                out=sc[:], in0=sc[:], scalar1=-1.0 / (D * D), scalar2=1.0, op0=ALU.mult, op1=ALU.add
+                out=sum_cos[:], in0=sum_cos[:], scalar1=-1.0 / (D * D), scalar2=1.0, op0=ALU.mult, op1=ALU.add
             )
             nc.vector.tensor_scalar(
-                out=gp[:], in0=sc[:], scalar1=cf32[:, 0:1], scalar2=1.0 / (2.0 * math.pi), op0=ALU.mult, op1=ALU.mult
+                out=gain[:], in0=sum_cos[:], scalar1=cf[:, 0:1], scalar2=1.0 / (2.0 * math.pi), op0=ALU.mult,
+                op1=ALU.mult,
             )
 
         with tc.tile_pool(name="workb", bufs=2) as workb, tc.tile_pool(name="stat", bufs=4) as stat, tc.psum_pool(
             name="ppsum", bufs=2
         ) as ppsum, tc.manual_schedule():
             p0 = {}
-            vs = {}
-            hh = {}
-            fa = {}
-            fb = {}
-            sa2 = {}
-            sb2 = {}
+            sine = {}
+            vers = {}
+            out_re = {}
+            cos_im = {}
+            rot_im = {}
+            rot_re = {}
             sums = {}
-            nmu = {}
-            sq = {}
-            rstd = {}
-            ot = {}
-            var = {}
+            neg_mean = {}
+            sq_dev = {}
+            var_eps = {}
+            inv_std = {}
+            turned_im = {}
 
             def valid(i):
                 return 0 <= i < NT
@@ -196,151 +203,173 @@ def tile_quantumcoherencelayer_kernel(
             def turned(i):
                 return 0 <= i < NT - 1
 
+            def product(i):
+                p0[i] = [ppsum.tile([P, BANK], F32, name="p0_%d" % n, tag="p0_%d" % n) for n in range(2)]
+                for n in range(2):
+                    for g in range(PASSES):
+                        nc.tensor.matmul_mx(
+                            out=p0[i][n][:],
+                            lhsT=x_codes[:, i, g * P : (g + 1) * P].bitcast(FP8X4),
+                            lhsT_scale=x_scales[:, i, g * P : (g + 1) * P],
+                            rhs=p_codes[:, g, n * BANK : (n + 1) * BANK].bitcast(FP8X4),
+                            rhs_scale=p_scales[:, g, n * BANK : (n + 1) * BANK],
+                            start=(g == 0),
+                            stop=(g == PASSES - 1),
+                        )
+
+            def reduce_range(i):
+                g_i = gain[:, i : i + 1]
+                nearest = workb.tile([P, D], I32, name="ki", tag="ki", bufs=1)
+                sine[i] = workb.tile([P, D], F32, name="vs", tag="vs")
+                for n in range(2):
+                    cols = slice(n * BANK, (n + 1) * BANK)
+                    nc.vector.tensor_scalar(
+                        out=nearest[:, cols], in0=p0[i][n][:], scalar1=g_i, scalar2=None, op0=ALU.mult
+                    )
+                for n in range(2):
+                    cols = slice(n * BANK, (n + 1) * BANK)
+                    nc.vector.scalar_tensor_tensor(
+                        out=sine[i][:, cols], in0=p0[i][n][:], scalar=g_i, in1=nearest[:, cols], op0=ALU.mult,
+                        op1=ALU.subtract,
+                    )
+
+            def two_sines(i):
+                vers[i] = workb.tile([P, D], F32, name="hh", tag="hh")
+                nc.scalar.activation(out=vers[i][:], in_=sine[i][:], func=ACT.Sin, scale=math.pi)
+                nc.scalar.activation(out=sine[i][:], in_=sine[i][:], func=ACT.Sin, scale=2.0 * math.pi)
+
+            def versine(i):
+                nc.scalar.activation(out=vers[i][:], in_=vers[i][:], func=ACT.Square, scale=math.sqrt(2.0))
+
+            def cosine_products_and_real_part(i):
+                out_re[i] = workb.tile([P, D], F32, name="fa", tag="fa", bufs=3)
+                cos_im[i] = workb.tile([P, D], F32, name="fb", tag="o%d" % (i % 4), bufs=1)
+                nc.vector.scalar_tensor_tensor(
+                    out=out_re[i][:], in0=vers[i][:], scalar=1.0, in1=unit_re[i][:], op0=ALU.subtract, op1=ALU.mult
+                )
+                nc.vector.scalar_tensor_tensor(
+                    out=cos_im[i][:], in0=vers[i][:], scalar=1.0, in1=unit_im_neg[i][:], op0=ALU.subtract, op1=ALU.mult
+                )
+                sums[i] = stat.tile([P, 2], F32, name="sums", tag="sums")
+                nc.vector.scalar_tensor_tensor(
+                    out=rot_re[i][:], in0=rot_re[i][:], scalar=1.0, in1=out_re[i][:], op0=ALU.mult, op1=ALU.subtract,
+                    accum_out=sums[i][:, 0:1],
+                )
+
+            def sine_product_re_on_vector(i):
+                rot_re[i] = workb.tile([P, D], F32, name="sb2", tag="sb2", bufs=3)
+                nc.vector.tensor_tensor(
+                    out=rot_re[i][:, POOL_COLS:D], in0=sine[i][:, POOL_COLS:D], in1=unit_im_neg[i][:, POOL_COLS:D],
+                    op=ALU.mult,
+                )
+
+            def normalise_im(i):
+                nc.vector.tensor_scalar(
+                    out=rot_im[i][:], in0=rot_im[i][:], scalar1=neg_mean[i][:, 1:2], scalar2=inv_std[i][:, 1:2],
+                    op0=ALU.add, op1=ALU.mult,
+                )
+
+            def imaginary_part_and_means(i):
+                nc.vector.scalar_tensor_tensor(
+                    out=rot_im[i][:], in0=rot_im[i][:], scalar=1.0, in1=cos_im[i][:], op0=ALU.mult, op1=ALU.add,
+                    accum_out=sums[i][:, 1:2],
+                )
+                neg_mean[i] = stat.tile([P, 2], F32, name="nmu", tag="nmu")
+                nc.vector.tensor_scalar(
+                    out=neg_mean[i][:], in0=sums[i][:], scalar1=-1.0 / D, scalar2=None, op0=ALU.mult
+                )
+
+            def variances(i):
+                sq_dev[i] = stat.tile([P, 2], F32, name="sq", tag="sq")
+                nc.scalar.activation(
+                    out=vers[i][:], in_=rot_re[i][:], func=ACT.Square, bias=neg_mean[i][:, 0:1], scale=1.0,
+                    accum_out=sq_dev[i][:, 0:1],
+                )
+                nc.scalar.activation(
+                    out=vers[i][:], in_=rot_im[i][:], func=ACT.Square, bias=neg_mean[i][:, 1:2], scale=1.0,
+                    accum_out=sq_dev[i][:, 1:2],
+                )
+                var_eps[i] = stat.tile([P, 2], F32, name="var", tag="var")
+                nc.scalar.activation(
+                    out=var_eps[i][:], in_=sq_dev[i][:], func=ACT.Identity, bias=eps_t[:, 0:1], scale=1.0 / D
+                )
+
+            def sine_products_on_gpsimd(i):
+                rot_im[i] = workb.tile([P, D], F32, name="sa2", tag="o%d" % ((i - 1) % 4), bufs=1)
+                nc.gpsimd.tensor_tensor(out=rot_im[i][:], in0=sine[i][:], in1=unit_re[i][:], op=ALU.mult)
+                nc.gpsimd.tensor_tensor(
+                    out=rot_re[i][:, 0:POOL_COLS], in0=sine[i][:, 0:POOL_COLS], in1=unit_im_neg[i][:, 0:POOL_COLS],
+                    op=ALU.mult,
+                )
+
+            def inverse_deviations(i):
+                inv_std[i] = stat.tile([P, 2], F32, name="rstd", tag="rstd")
+                nc.gpsimd.tensor_tensor(out=inv_std[i][:], in0=var_eps[i][:], in1=neghalf[:], op=ALU.pow)
+
+            def scale_shift(dst, src, i, c):
+                nc.vector.scalar_tensor_tensor(
+                    out=dst[:], in0=src[:], scalar=neg_mean[i][:, c : c + 1], in1=w_ps[:], op0=ALU.add, op1=ALU.mult
+                )
+                nc.vector.scalar_tensor_tensor(
+                    out=dst[:], in0=dst[:], scalar=inv_std[i][:, c : c + 1], in1=b_ps[:], op0=ALU.mult, op1=ALU.add
+                )
+
             def there(i, half):
-                t1 = ppsum.tile([P, HALF], F32, name="t1", tag="t1", bufs=1)
+                t1 = ppsum.tile([P, BANK], F32, name="t1", tag="t1", bufs=1)
                 for jj in range(4):
                     j = 4 * half + jj
                     nc.tensor.transpose(
-                        out=t1[:, jj * P : (jj + 1) * P], in_=sa2[i][:, j * P : (j + 1) * P], identity=ident[:]
+                        out=t1[:, jj * P : (jj + 1) * P], in_=rot_im[i][:, j * P : (j + 1) * P], identity=ident[:]
                     )
                 for jj in range(4):
                     j = 4 * half + jj
                     nc.scalar.activation(
-                        out=ot[i][:, j, :], in_=t1[:, jj * P : (jj + 1) * P], func=ACT.Identity,
-                        bias=wbt[:, 8 + j : 9 + j], scale=wbt[:, j : j + 1],
+                        out=turned_im[i][:, j, :], in_=t1[:, jj * P : (jj + 1) * P], func=ACT.Identity,
+                        bias=wb_cols[:, BLOCKS + j : BLOCKS + j + 1], scale=wb_cols[:, j : j + 1],
                     )
 
             def back(i, half):
-                t2 = ppsum.tile([P, HALF], F32, name="t2", tag="t2", bufs=1)
+                t2 = ppsum.tile([P, BANK], F32, name="t2", tag="t2", bufs=1)
                 for jj in range(4):
                     j = 4 * half + jj
-                    nc.tensor.transpose(out=t2[:, jj * P : (jj + 1) * P], in_=ot[i][:, j, :], identity=ident[:])
-                nc.scalar.copy(out=sa2[i][:, half * HALF : (half + 1) * HALF], in_=t2[:])
+                    nc.tensor.transpose(out=t2[:, jj * P : (jj + 1) * P], in_=turned_im[i][:, j, :], identity=ident[:])
+                nc.scalar.copy(out=rot_im[i][:, half * BANK : (half + 1) * BANK], in_=t2[:])
 
             for k in range(-3, NT + 1):
-                i = k + 3
-                if valid(i):
-                    p0[i] = [ppsum.tile([P, HALF], F32, name="p0_%d" % n, tag="p0_%d" % n) for n in range(2)]
-                    for n in range(2):
-                        for g in range(2):
-                            nc.tensor.matmul_mx(
-                                out=p0[i][n][:],
-                                lhsT=xcodes[:, i, g * P : (g + 1) * P].bitcast(FP8X4),
-                                lhsT_scale=xscales[:, i, g * P : (g + 1) * P],
-                                rhs=pcodes[:, g, n * HALF : (n + 1) * HALF].bitcast(FP8X4),
-                                rhs_scale=pscales[:, g, n * HALF : (n + 1) * HALF],
-                                start=(g == 0),
-                                stop=(g == 1),
-                            )
                 if valid(k + 1):
-                    i = k + 1
-                    hh[i] = workb.tile([P, D], F32, name="hh", tag="hh")
-                    nc.scalar.activation(out=hh[i][:], in_=vs[i][:], func=ACT.Sin, scale=math.pi)
-                    nc.scalar.activation(out=vs[i][:], in_=vs[i][:], func=ACT.Sin, scale=2.0 * math.pi)
-                i = k
-                if valid(i):
-                    fa[i] = workb.tile([P, D], F32, name="fa", tag="fa", bufs=3)
-                    fb[i] = workb.tile([P, D], F32, name="fb", tag="o%d" % (i % 4), bufs=1)
-                    nc.vector.scalar_tensor_tensor(
-                        out=fa[i][:], in0=hh[i][:], scalar=1.0, in1=cr_all[i][:], op0=ALU.subtract, op1=ALU.mult
-                    )
-                    nc.vector.scalar_tensor_tensor(
-                        out=fb[i][:], in0=hh[i][:], scalar=1.0, in1=nci_all[i][:], op0=ALU.subtract, op1=ALU.mult
-                    )
-                i = k - 1
-                if turned(i):
-                    nc.vector.tensor_scalar(
-                        out=sa2[i][:], in0=sa2[i][:], scalar1=nmu[i][:, 1:2], scalar2=rstd[i][:, 1:2], op0=ALU.add,
-                        op1=ALU.mult,
-                    )
-                i = k
-                if valid(i):
-                    sums[i] = stat.tile([P, 2], F32, name="sums", tag="sums")
-                    nc.vector.scalar_tensor_tensor(
-                        out=sb2[i][:], in0=sb2[i][:], scalar=1.0, in1=fa[i][:], op0=ALU.mult, op1=ALU.subtract,
-                        accum_out=sums[i][:, 0:1],
-                    )
-                if valid(k + 1):
-                    sb2[k + 1] = workb.tile([P, D], F32, name="sb2", tag="sb2", bufs=3)
-                    nc.vector.tensor_tensor(
-                        out=sb2[k + 1][:, POOL_COLS:D], in0=vs[k + 1][:, POOL_COLS:D], in1=nci_all[k + 1][:, POOL_COLS:D],
-                        op=ALU.mult,
-                    )
-                if valid(i):
-                    nc.vector.scalar_tensor_tensor(
-                        out=sa2[i][:], in0=sa2[i][:], scalar=1.0, in1=fb[i][:], op0=ALU.mult, op1=ALU.add,
-                        accum_out=sums[i][:, 1:2],
-                    )
-                    nmu[i] = stat.tile([P, 2], F32, name="nmu", tag="nmu")
-                    nc.vector.tensor_scalar(out=nmu[i][:], in0=sums[i][:], scalar1=-1.0 / D, scalar2=None, op0=ALU.mult)
+                    two_sines(k + 1)
                 if turned(k - 2):
                     back(k - 2, 1)
-                    nc.sync.dma_start(out=o1_d[k - 2], in_=sa2[k - 2][:])
-                if turned(k - 1):
-                    ot[k - 1] = workb.tile([P, 8, P], F32, name="ot", tag="ot", bufs=1)
-                    there(k - 1, 0)
+                    nc.sync.dma_start(out=o1_d[k - 2], in_=rot_im[k - 2][:])
+                if valid(k):
+                    cosine_products_and_real_part(k)
                 if valid(k + 1):
-                    i = k + 1
-                    nc.scalar.activation(out=hh[i][:], in_=hh[i][:], func=ACT.Square, scale=math.sqrt(2.0))
-                i = k
-                if valid(i):
-                    sq[i] = stat.tile([P, 2], F32, name="sq", tag="sq")
-                    nc.scalar.activation(
-                        out=hh[i][:], in_=sb2[i][:], func=ACT.Square, bias=nmu[i][:, 0:1], scale=1.0,
-                        accum_out=sq[i][:, 0:1],
-                    )
-                    nc.scalar.activation(
-                        out=hh[i][:], in_=sa2[i][:], func=ACT.Square, bias=nmu[i][:, 1:2], scale=1.0,
-                        accum_out=sq[i][:, 1:2],
-                    )
-                    var[i] = stat.tile([P, 2], F32, name="var", tag="var")
-                    nc.scalar.activation(out=var[i][:], in_=sq[i][:], func=ACT.Identity, bias=eps_t[:, 0:1], scale=1.0 / D)
+                    sine_product_re_on_vector(k + 1)
+                if turned(k - 1):
+                    normalise_im(k - 1)
+                if valid(k):
+                    imaginary_part_and_means(k)
+                if valid(k + 1):
+                    versine(k + 1)
+                if turned(k - 1):
+                    turned_im[k - 1] = workb.tile([P, BLOCKS, P], F32, name="ot", tag="ot", bufs=1)
+                    there(k - 1, 0)
+                if valid(k + 3):
+                    product(k + 3)
+                if valid(k):
+                    variances(k)
                 if turned(k - 1):
                     back(k - 1, 0)
                     there(k - 1, 1)
-                i = k - 1
-                if valid(i):
-                    nc.vector.scalar_tensor_tensor(
-                        out=fa[i][:], in0=sb2[i][:], scalar=nmu[i][:, 0:1], in1=wps[:], op0=ALU.add, op1=ALU.mult
-                    )
-                    nc.vector.scalar_tensor_tensor(
-                        out=fa[i][:], in0=fa[i][:], scalar=rstd[i][:, 0:1], in1=bps[:], op0=ALU.mult, op1=ALU.add
-                    )
-                    nc.sync.dma_start(out=o0_d[i], in_=fa[i][:])
-                if i == NT - 1:
-                    nc.vector.scalar_tensor_tensor(
-                        out=sa2[i][:], in0=sa2[i][:], scalar=nmu[i][:, 1:2], in1=wps[:], op0=ALU.add, op1=ALU.mult
-                    )
-                    nc.vector.scalar_tensor_tensor(
-                        out=sa2[i][:], in0=sa2[i][:], scalar=rstd[i][:, 1:2], in1=bps[:], op0=ALU.mult, op1=ALU.add
-                    )
-                    nc.sync.dma_start(out=o1_d[i], in_=sa2[i][:])
-                i = k + 1
-                if valid(i):
-                    sa2[i] = workb.tile([P, D], F32, name="sa2", tag="o%d" % ((i - 1) % 4), bufs=1)
-                    nc.gpsimd.tensor_tensor(out=sa2[i][:], in0=vs[i][:], in1=cr_all[i][:], op=ALU.mult)
-                i = k
-                if valid(i):
-                    rstd[i] = stat.tile([P, 2], F32, name="rstd", tag="rstd")
-                    nc.gpsimd.tensor_tensor(out=rstd[i][:], in0=var[i][:], in1=neghalf[:], op=ALU.pow)
-                i = k + 1
-                if valid(i):
-                    nc.gpsimd.tensor_tensor(
-                        out=sb2[i][:, 0:POOL_COLS], in0=vs[i][:, 0:POOL_COLS], in1=nci_all[i][:, 0:POOL_COLS], op=ALU.mult
-                    )
-                i = k + 2
-                if valid(i):
-                    g_i = gp[:, i : i + 1]
-                    ki = workb.tile([P, D], I32, name="ki", tag="ki", bufs=1)
-                    vs[i] = workb.tile([P, D], F32, name="vs", tag="vs")
-                    for n in range(2):
-                        cols = slice(n * HALF, (n + 1) * HALF)
-                        nc.vector.tensor_scalar(
-                            out=ki[:, cols], in0=p0[i][n][:], scalar1=g_i, scalar2=None, op0=ALU.mult
-                        )
-                    for n in range(2):
-                        cols = slice(n * HALF, (n + 1) * HALF)
-                        nc.vector.scalar_tensor_tensor(
-                            out=vs[i][:, cols], in0=p0[i][n][:], scalar=g_i, in1=ki[:, cols], op0=ALU.mult,
-                            op1=ALU.subtract,
-                        )
+                if valid(k - 1):
+                    scale_shift(out_re[k - 1], rot_re[k - 1], k - 1, 0)
+                    nc.sync.dma_start(out=o0_d[k - 1], in_=out_re[k - 1][:])
+                if k - 1 == NT - 1:
+                    scale_shift(rot_im[k - 1], rot_im[k - 1], k - 1, 1)
+                    nc.sync.dma_start(out=o1_d[k - 1], in_=rot_im[k - 1][:])
+                if valid(k + 1):
+                    sine_products_on_gpsimd(k + 1)
+                if valid(k):
+                    inverse_deviations(k)
+                if valid(k + 2):
+                    reduce_range(k + 2)

import math
from contextlib import ExitStack

import concourse.mybir as mybir
from concourse.masks import make_identity

F32 = mybir.dt.float32
BF16 = mybir.dt.bfloat16
I32 = mybir.dt.int32
U32 = mybir.dt.uint32
U8 = mybir.dt.uint8
FP8X4 = mybir.dt.float8_e4m3fn_x4
ACT = mybir.ActivationFunctionType
ALU = mybir.AluOpType

P = 128
D = 1024
ROWS = 2048
NT = ROWS // P
BANK = 512
PASSES = D // 512
BLOCKS = D // P
EPS = 1e-8
POOL_COLS = 768
FLOPS = 2 * ROWS * D * D


def tile_quantumcoherencelayer_kernel(
    tc, x_real, x_imag, phase_matrix, coherence_factor, ln_weight, ln_bias, out_0, out_1
):
    nc = tc.nc
    xr_d = x_real.flatten_outer_dims().rearrange("(t p) d -> t p d", p=P)
    xi_d = x_imag.flatten_outer_dims().rearrange("(t p) d -> t p d", p=P)
    o0_d = out_0.flatten_outer_dims().rearrange("(t p) d -> t p d", p=P)
    o1_d = out_1.flatten_outer_dims().rearrange("(t p) d -> t p d", p=P)

    with ExitStack() as ctx:
        keep = ctx.enter_context(tc.tile_pool(name="keep", bufs=1))
        cpsum = ctx.enter_context(tc.psum_pool(name="cpsum", bufs=1))

        ident = keep.tile([P, P], F32)
        make_identity(nc, ident[:])
        eps_t = keep.tile([P, 1], F32)
        nc.vector.memset(eps_t[:], EPS)
        neghalf = keep.tile([P, 2], F32)
        nc.vector.memset(neghalf[:], -0.5)

        cf_bf = keep.tile([P, 1], BF16)
        with nc.allow_non_contiguous_dma(reason="one bfloat16 scalar to every partition"):
            nc.scalar.dma_start(out=cf_bf[:], in_=coherence_factor.partition_broadcast(P))
        cf = keep.tile([P, 1], F32)
        nc.vector.tensor_copy(out=cf[:], in_=cf_bf[:])

        p_codes = keep.tile([P, PASSES, D], U32, align_bytes=64)
        p_scales = keep.tile([P, PASSES, D], U8, align_bytes=64)
        x_codes = keep.tile([P, NT, PASSES * P], U32, align_bytes=64)
        x_scales = keep.tile([P, NT, PASSES * P], U8, align_bytes=64)
        sum_cos = keep.tile([P, NT], F32)
        sum_sin = keep.tile([P, NT], F32)
        gain = keep.tile([P, NT], F32)
        wb_cols = keep.tile([P, 2 * BLOCKS], F32)
        unit_re = [keep.tile([P, D], F32, name="cr%d" % i) for i in range(NT)]
        unit_im_neg = [keep.tile([P, D], F32, name="nci%d" % i) for i in range(NT)]

        w_ps = cpsum.tile([P, D], BF16)
        b_ps = cpsum.tile([P, D], BF16)

        with tc.tile_pool(name="stage", bufs=1) as stage, tc.tile_pool(name="xin", bufs=3) as xin, tc.tile_pool(
            name="worka", bufs=2
        ) as worka, tc.psum_pool(name="tpsum", bufs=2) as tpsum:
            rows = stage.tile([P, 2 * D], BF16)
            nc.vector.memset(rows[:], 0.0)
            nc.scalar.dma_start(out=rows[0:1, 0:D], in_=ln_weight.rearrange("(o d) -> o d", o=1))
            nc.scalar.dma_start(out=rows[0:1, D : 2 * D], in_=ln_bias.rearrange("(o d) -> o d", o=1))
            ones = stage.tile([P, P], BF16)
            nc.vector.memset(ones[:], 1.0)
            for h in range(2):
                nc.tensor.matmul(
                    out=w_ps[:, h * BANK : (h + 1) * BANK],
                    lhsT=ones[:],
                    rhs=rows[:, h * BANK : (h + 1) * BANK],
                    start=True,
                    stop=True,
                )
            for h in range(2):
                nc.tensor.matmul(
                    out=b_ps[:, h * BANK : (h + 1) * BANK],
                    lhsT=ones[:],
                    rhs=rows[:, D + h * BANK : D + (h + 1) * BANK],
                    start=True,
                    stop=True,
                )

            wb = stage.tile([P, P], BF16)
            nc.vector.memset(wb[:], 0.0)
            nc.scalar.dma_start(out=wb[0:BLOCKS, :], in_=ln_weight.rearrange("(j p) -> j p", p=P))
            nc.scalar.dma_start(out=wb[BLOCKS : 2 * BLOCKS, :], in_=ln_bias.rearrange("(j p) -> j p", p=P))
            wb32 = stage.tile([P, P], F32)
            nc.vector.tensor_copy(out=wb32[:], in_=wb[:])
            wbt_ps = tpsum.tile([P, BANK], F32, tag="xt")
            nc.tensor.transpose(out=wbt_ps[:, 0:P], in_=wb32[:], identity=ident[:])
            nc.vector.tensor_copy(out=wb_cols[:], in_=wbt_ps[:, 0 : 2 * BLOCKS])

            for i in range(NT):
                xr = xin.tile([P, D], BF16, tag="xr")
                nc.sync.dma_start(out=xr[:], in_=xr_d[i])
                xi = xin.tile([P, D], BF16, tag="xi")
                nc.sync.dma_start(out=xi[:], in_=xi_d[i])

                if i == 1:
                    for g in range(PASSES):
                        raw = stage.tile([P, 4, D], BF16, tag="raw")
                        for u in range(2):
                            k0 = 512 * g + 256 * u
                            nc.sync.dma_start(
                                out=raw[:, 2 * u : 2 * u + 2, :],
                                in_=phase_matrix[k0 : k0 + 256, :].rearrange("(q e) c -> q e c", e=2),
                            )
                        pg = stage.tile([P, D, 4], BF16, tag="pg", align_bytes=64)
                        nc.vector.tensor_copy(
                            out=pg[:].rearrange("p (c i) t -> p c t i", i=4),
                            in_=raw[:].rearrange("p t (c i) -> p c t i", i=4),
                        )
                        nc.vector.quantize_mx(
                            out=p_codes[:, g, :].bitcast(FP8X4),
                            scales=p_scales[:, g, :],
                            in_=pg[:].rearrange("p c t -> p (c t)"),
                        )

                xt = tpsum.tile([P, BANK], F32, tag="xt")
                xw = xr[:].bitcast(F32)
                for j in range(4):
                    nc.tensor.transpose(out=xt[:, j * P : (j + 1) * P], in_=xw[:, j * P : (j + 1) * P], identity=ident[:])
                grouped = worka.tile([P, PASSES, P, 4], BF16, tag="grouped", align_bytes=64)
                nc.scalar.copy(
                    out=grouped[:].bitcast(F32),
                    in_=xt[:].rearrange("p (g u r) -> p g r u", g=PASSES, u=2),
                )

                inv_r = worka.tile([P, D], F32, tag="sa")
                scr_a = worka.tile([P, D], F32, tag="sb")
                inv_n = worka.tile([P, D], F32, tag="sr")
                scr_b = worka.tile([P, D], F32, tag="si")
                nc.scalar.activation(out=inv_r[:], in_=xr[:], func=ACT.Square, bias=eps_t[:, 0:1], scale=1.0)
                nc.scalar.activation(out=scr_a[:], in_=xi[:], func=ACT.Square, bias=eps_t[:, 0:1], scale=1.0)
                nc.scalar.activation(out=inv_n[:], in_=xr[:], func=ACT.Square)
                nc.scalar.activation(out=scr_b[:], in_=xi[:], func=ACT.Square)
                nc.vector.tensor_tensor(out=inv_r[:], in0=inv_r[:], in1=scr_a[:], op=ALU.add)
                nc.vector.tensor_tensor(out=inv_n[:], in0=inv_n[:], in1=scr_b[:], op=ALU.add)
                nc.vector.quantize_mx(
                    out=x_codes[:, i, :].bitcast(FP8X4),
                    scales=x_scales[:, i, :],
                    in_=grouped[:].rearrange("p g r t -> p (g r t)"),
                )
                nc.scalar.activation(out=inv_r[:], in_=inv_r[:], func=ACT.Abs_reciprocal_sqrt)
                nc.scalar.activation(
                    out=inv_n[:], in_=inv_n[:], func=ACT.Abs_reciprocal_sqrt, bias=eps_t[:, 0:1], scale=1.0
                )
                nc.vector.scalar_tensor_tensor(
                    out=scr_a[:], in0=xr[:], scalar=EPS, in1=inv_r[:], op0=ALU.add, op1=ALU.mult,
                    accum_out=sum_cos[:, i : i + 1],
                )
                nc.vector.scalar_tensor_tensor(
                    out=scr_b[:], in0=xi[:], scalar=EPS, in1=inv_r[:], op0=ALU.add, op1=ALU.mult,
                    accum_out=sum_sin[:, i : i + 1],
                )
                nc.vector.tensor_tensor(out=unit_re[i][:], in0=xr[:], in1=inv_n[:], op=ALU.mult)
                nc.vector.scalar_tensor_tensor(
                    out=unit_im_neg[i][:], in0=xi[:], scalar=-1.0, in1=inv_n[:], op0=ALU.mult, op1=ALU.mult
                )

            nc.vector.tensor_tensor(out=sum_cos[:], in0=sum_cos[:], in1=sum_cos[:], op=ALU.mult)
            nc.vector.tensor_tensor(out=sum_sin[:], in0=sum_sin[:], in1=sum_sin[:], op=ALU.mult)
            nc.vector.tensor_tensor(out=sum_cos[:], in0=sum_cos[:], in1=sum_sin[:], op=ALU.add)
            nc.vector.tensor_scalar(
                out=sum_cos[:], in0=sum_cos[:], scalar1=-1.0 / (D * D), scalar2=1.0, op0=ALU.mult, op1=ALU.add
            )
            nc.vector.tensor_scalar(
                out=gain[:], in0=sum_cos[:], scalar1=cf[:, 0:1], scalar2=1.0 / (2.0 * math.pi), op0=ALU.mult,
                op1=ALU.mult,
            )

        with tc.tile_pool(name="workb", bufs=2) as workb, tc.tile_pool(name="stat", bufs=4) as stat, tc.psum_pool(
            name="ppsum", bufs=2
        ) as ppsum, tc.manual_schedule():
            p0 = {}
            sine = {}
            vers = {}
            out_re = {}
            cos_im = {}
            rot_im = {}
            rot_re = {}
            sums = {}
            neg_mean = {}
            sq_dev = {}
            var_eps = {}
            inv_std = {}
            turned_im = {}

            def valid(i):
                return 0 <= i < NT

            def turned(i):
                return 0 <= i < NT - 1

            def product(i):
                p0[i] = [ppsum.tile([P, BANK], F32, name="p0_%d" % n, tag="p0_%d" % n) for n in range(2)]
                for n in range(2):
                    for g in range(PASSES):
                        nc.tensor.matmul_mx(
                            out=p0[i][n][:],
                            lhsT=x_codes[:, i, g * P : (g + 1) * P].bitcast(FP8X4),
                            lhsT_scale=x_scales[:, i, g * P : (g + 1) * P],
                            rhs=p_codes[:, g, n * BANK : (n + 1) * BANK].bitcast(FP8X4),
                            rhs_scale=p_scales[:, g, n * BANK : (n + 1) * BANK],
                            start=(g == 0),
                            stop=(g == PASSES - 1),
                        )

            def reduce_range(i):
                g_i = gain[:, i : i + 1]
                nearest = workb.tile([P, D], I32, name="ki", tag="ki", bufs=1)
                sine[i] = workb.tile([P, D], F32, name="vs", tag="vs")
                for n in range(2):
                    cols = slice(n * BANK, (n + 1) * BANK)
                    nc.vector.tensor_scalar(
                        out=nearest[:, cols], in0=p0[i][n][:], scalar1=g_i, scalar2=None, op0=ALU.mult
                    )
                for n in range(2):
                    cols = slice(n * BANK, (n + 1) * BANK)
                    nc.vector.scalar_tensor_tensor(
                        out=sine[i][:, cols], in0=p0[i][n][:], scalar=g_i, in1=nearest[:, cols], op0=ALU.mult,
                        op1=ALU.subtract,
                    )

            def two_sines(i):
                vers[i] = workb.tile([P, D], F32, name="hh", tag="hh")
                nc.scalar.activation(out=vers[i][:], in_=sine[i][:], func=ACT.Sin, scale=math.pi)
                nc.scalar.activation(out=sine[i][:], in_=sine[i][:], func=ACT.Sin, scale=2.0 * math.pi)

            def versine(i):
                nc.scalar.activation(out=vers[i][:], in_=vers[i][:], func=ACT.Square, scale=math.sqrt(2.0))

            def cosine_products_and_real_part(i):
                out_re[i] = workb.tile([P, D], F32, name="fa", tag="fa", bufs=3)
                cos_im[i] = workb.tile([P, D], F32, name="fb", tag="o%d" % (i % 4), bufs=1)
                nc.vector.scalar_tensor_tensor(
                    out=out_re[i][:], in0=vers[i][:], scalar=1.0, in1=unit_re[i][:], op0=ALU.subtract, op1=ALU.mult
                )
                nc.vector.scalar_tensor_tensor(
                    out=cos_im[i][:], in0=vers[i][:], scalar=1.0, in1=unit_im_neg[i][:], op0=ALU.subtract, op1=ALU.mult
                )
                sums[i] = stat.tile([P, 2], F32, name="sums", tag="sums")
                nc.vector.scalar_tensor_tensor(
                    out=rot_re[i][:], in0=rot_re[i][:], scalar=1.0, in1=out_re[i][:], op0=ALU.mult, op1=ALU.subtract,
                    accum_out=sums[i][:, 0:1],
                )

            def sine_product_re_on_vector(i):
                rot_re[i] = workb.tile([P, D], F32, name="sb2", tag="sb2", bufs=3)
                nc.vector.tensor_tensor(
                    out=rot_re[i][:, POOL_COLS:D], in0=sine[i][:, POOL_COLS:D], in1=unit_im_neg[i][:, POOL_COLS:D],
                    op=ALU.mult,
                )

            def normalise_im(i):
                nc.vector.tensor_scalar(
                    out=rot_im[i][:], in0=rot_im[i][:], scalar1=neg_mean[i][:, 1:2], scalar2=inv_std[i][:, 1:2],
                    op0=ALU.add, op1=ALU.mult,
                )

            def imaginary_part_and_means(i):
                nc.vector.scalar_tensor_tensor(
                    out=rot_im[i][:], in0=rot_im[i][:], scalar=1.0, in1=cos_im[i][:], op0=ALU.mult, op1=ALU.add,
                    accum_out=sums[i][:, 1:2],
                )
                neg_mean[i] = stat.tile([P, 2], F32, name="nmu", tag="nmu")
                nc.vector.tensor_scalar(
                    out=neg_mean[i][:], in0=sums[i][:], scalar1=-1.0 / D, scalar2=None, op0=ALU.mult
                )

            def variances(i):
                sq_dev[i] = stat.tile([P, 2], F32, name="sq", tag="sq")
                nc.scalar.activation(
                    out=vers[i][:], in_=rot_re[i][:], func=ACT.Square, bias=neg_mean[i][:, 0:1], scale=1.0,
                    accum_out=sq_dev[i][:, 0:1],
                )
                nc.scalar.activation(
                    out=vers[i][:], in_=rot_im[i][:], func=ACT.Square, bias=neg_mean[i][:, 1:2], scale=1.0,
                    accum_out=sq_dev[i][:, 1:2],
                )
                var_eps[i] = stat.tile([P, 2], F32, name="var", tag="var")
                nc.scalar.activation(
                    out=var_eps[i][:], in_=sq_dev[i][:], func=ACT.Identity, bias=eps_t[:, 0:1], scale=1.0 / D
                )

            def sine_products_on_gpsimd(i):
                rot_im[i] = workb.tile([P, D], F32, name="sa2", tag="o%d" % ((i - 1) % 4), bufs=1)
                nc.gpsimd.tensor_tensor(out=rot_im[i][:], in0=sine[i][:], in1=unit_re[i][:], op=ALU.mult)
                nc.gpsimd.tensor_tensor(
                    out=rot_re[i][:, 0:POOL_COLS], in0=sine[i][:, 0:POOL_COLS], in1=unit_im_neg[i][:, 0:POOL_COLS],
                    op=ALU.mult,
                )

            def inverse_deviations(i):
                inv_std[i] = stat.tile([P, 2], F32, name="rstd", tag="rstd")
                nc.gpsimd.tensor_tensor(out=inv_std[i][:], in0=var_eps[i][:], in1=neghalf[:], op=ALU.pow)

            def scale_shift(dst, src, i, c):
                nc.vector.scalar_tensor_tensor(
                    out=dst[:], in0=src[:], scalar=neg_mean[i][:, c : c + 1], in1=w_ps[:], op0=ALU.add, op1=ALU.mult
                )
                nc.vector.scalar_tensor_tensor(
                    out=dst[:], in0=dst[:], scalar=inv_std[i][:, c : c + 1], in1=b_ps[:], op0=ALU.mult, op1=ALU.add
                )

            def there(i, half):
                t1 = ppsum.tile([P, BANK], F32, name="t1", tag="t1", bufs=1)
                for jj in range(4):
                    j = 4 * half + jj
                    nc.tensor.transpose(
                        out=t1[:, jj * P : (jj + 1) * P], in_=rot_im[i][:, j * P : (j + 1) * P], identity=ident[:]
                    )
                for jj in range(4):
                    j = 4 * half + jj
                    nc.scalar.activation(
                        out=turned_im[i][:, j, :], in_=t1[:, jj * P : (jj + 1) * P], func=ACT.Identity,
                        bias=wb_cols[:, BLOCKS + j : BLOCKS + j + 1], scale=wb_cols[:, j : j + 1],
                    )

            def back(i, half):
                t2 = ppsum.tile([P, BANK], F32, name="t2", tag="t2", bufs=1)
                for jj in range(4):
                    j = 4 * half + jj
                    nc.tensor.transpose(out=t2[:, jj * P : (jj + 1) * P], in_=turned_im[i][:, j, :], identity=ident[:])
                nc.scalar.copy(out=rot_im[i][:, half * BANK : (half + 1) * BANK], in_=t2[:])

            for k in range(-3, NT + 1):
                if valid(k + 1):
                    two_sines(k + 1)
                if turned(k - 2):
                    back(k - 2, 1)
                    nc.sync.dma_start(out=o1_d[k - 2], in_=rot_im[k - 2][:])
                if valid(k):
                    cosine_products_and_real_part(k)
                if valid(k + 1):
                    sine_product_re_on_vector(k + 1)
                if turned(k - 1):
                    normalise_im(k - 1)
                if valid(k):
                    imaginary_part_and_means(k)
                if valid(k + 1):
                    versine(k + 1)
                if turned(k - 1):
                    turned_im[k - 1] = workb.tile([P, BLOCKS, P], F32, name="ot", tag="ot", bufs=1)
                    there(k - 1, 0)
                if valid(k + 3):
                    product(k + 3)
                if valid(k):
                    variances(k)
                if turned(k - 1):
                    back(k - 1, 0)
                    there(k - 1, 1)
                if valid(k - 1):
                    scale_shift(out_re[k - 1], rot_re[k - 1], k - 1, 0)
                    nc.sync.dma_start(out=o0_d[k - 1], in_=out_re[k - 1][:])
                if k - 1 == NT - 1:
                    scale_shift(rot_im[k - 1], rot_im[k - 1], k - 1, 1)
                    nc.sync.dma_start(out=o1_d[k - 1], in_=rot_im[k - 1][:])
                if valid(k + 1):
                    sine_products_on_gpsimd(k + 1)
                if valid(k):
                    inverse_deviations(k)
                if valid(k + 2):
                    reduce_range(k + 2)
